import numpy as np
import ml_dtypes


def mxq(x, axis, fmt="e4m3"):
    dtype, down = {"e4m3": (ml_dtypes.float8_e4m3fn, 7), "e5m2": (ml_dtypes.float8_e5m2, 14)}[fmt]
    v = np.moveaxis(np.asarray(x, np.float32).astype(ml_dtypes.bfloat16).astype(np.float64), axis, -1)
    blocks = v.reshape(v.shape[:-1] + (-1, 32))
    amax = np.abs(blocks).max(-1, keepdims=True)
    byte = np.maximum(np.where(amax > 0, np.frexp(amax)[1] - 1 + 127, 0) - down, 1)
    scale = np.exp2(byte - 127.0)
    codes = (blocks / scale).astype(np.float32).astype(dtype).astype(np.float64)
    return np.moveaxis((codes * scale).reshape(v.shape), -1, axis)


WIDE = False


def mx_kscale(k):
    if not WIDE:
        return np.ones(k)
    levels = np.array([10, -10, 5, -5, 0])
    a = np.random.permutation(np.resize(levels, k // 512 * 4)).reshape(k // 512, 4)
    idx = np.arange(k)
    return np.exp2(a[idx // 512, idx % 128 // 32])


BF16 = ml_dtypes.bfloat16


def bf(x):
    return np.asarray(x, np.float32).astype(BF16)


def f64(x):
    return np.asarray(x).astype(np.float64)


B, D_IN, H1, H2, LAT, NQ, NL, NA = 8192, 4096, 2048, 512, 512, 512, 2, 3


def circuit(th, P):
    ar, ai = np.cos(0.5 * th), np.zeros_like(th)
    br, bi = np.sin(0.5 * th), np.zeros_like(th)
    for l in range(NL):
        rx, ry, rz = P[l].T
        c, s = np.cos(0.5 * rx), np.sin(0.5 * rx)
        ar, ai, br, bi = c * ar + s * bi, c * ai - s * br, s * ai + c * br, c * bi - s * ar
        c, s = np.cos(0.5 * ry), np.sin(0.5 * ry)
        ar, ai, br, bi = c * ar - s * br, c * ai - s * bi, s * ar + c * br, s * ai + c * bi
        c, s = np.cos(0.5 * rz), np.sin(0.5 * rz)
        ar, ai, br, bi = c * ar + s * ai, c * ai - s * ar, c * br - s * bi, c * bi + s * br
    return (ar * ar + ai * ai) - (br * br + bi * bi)


def setup_inputs():
    s = mx_kscale(H2)
    return {"h_enc2": bf(np.maximum(np.random.standard_normal((B, H2)), 0.0) * s),
            "We3": bf(np.random.standard_normal((NQ, H2)) * 1.4 / np.sqrt(H2) / s),
            "be3": bf(np.random.standard_normal(NQ) * 0.3),
            "P": bf(np.random.standard_normal((NL, NQ, NA))),
            "Wd1": bf(np.random.standard_normal((H2, NQ)) * 1.7 / np.sqrt(NQ)),
            "bd1": bf(np.random.standard_normal(H2) * 0.3)}


def reference(h_enc2, We3, be3, P, Wd1, bd1):
    th = (mxq(f64(h_enc2), 1, "e4m3") @ mxq(f64(We3), 1, "e4m3").T) + f64(be3)
    z = circuit(th, f64(P))
    return np.maximum((mxq(z, 1, "e4m3") @ mxq(f64(Wd1), 1, "e4m3").T) + f64(bd1), 0.0)

@@ -1,0 +1,254 @@
+import math
+
+import concourse.mybir as mybir
+from concourse.masks import make_identity
+
+F32 = mybir.dt.float32
+BF16 = mybir.dt.bfloat16
+I32 = mybir.dt.int32
+U32 = mybir.dt.uint32
+U8 = mybir.dt.uint8
+FP8X4 = mybir.dt.float8_e4m3fn_x4
+ALU = mybir.AluOpType
+ACT = mybir.ActivationFunctionType
+
+P = 128
+PACK = 4
+ROWS = 8192
+WIDTH = 512
+CHUNK = 512
+BLOCKS = CHUNK // P
+CHUNKS = ROWS // CHUNK
+LAYERS = 2
+RX, RY, RZ = 0, 1, 2
+
+TWO_PI = 2.0 * math.pi
+INV_TWO_PI = 1.0 / TWO_PI
+HALF_PI = 0.5 * math.pi
+ROUND = 12582912.0
+TINY = 1e-30
+FLT_MAX = 3.4028234663852886e38
+
+FLOPS = 2 * 2 * ROWS * WIDTH * WIDTH
+
+
+def transpose_and_quantise(nc, psum, stage, identity, word_block, codes, scales):
+    grouped = stage.tile([P, BLOCKS * P * PACK], BF16, align_bytes=64, tag="grouped")
+    grouped_words = grouped[:].bitcast(F32).rearrange("p (n c u) -> p n c u", n=BLOCKS, u=2)
+    for half in range(2):
+        flipped = psum.tile([P, 2, 2, P], F32, tag="flipped")
+        for n in range(2):
+            for u in range(2):
+                nc.tensor.transpose(flipped[:, n, u, :], word_block(2 * half + n, u), identity[:])
+        nc.scalar.copy(
+            out=grouped_words[:, 2 * half : 2 * half + 2, :, :],
+            in_=flipped[:].rearrange("p n u c -> p n c u"),
+        )
+    nc.vector.quantize_mx(out=codes.bitcast(FP8X4), scales=scales, in_=grouped[:])
+
+
+def qubit_constants(nc, consts, params, be3):
+    def small(name):
+        return consts.tile([P, PACK], F32, name=name)
+
+    def mul(out, a, b):
+        nc.vector.tensor_tensor(out=out, in0=a, in1=b, op=ALU.mult)
+
+    def add(out, a, b):
+        nc.vector.tensor_tensor(out=out, in0=a, in1=b, op=ALU.add)
+
+    def sub(out, a, b):
+        nc.vector.tensor_tensor(out=out, in0=a, in1=b, op=ALU.subtract)
+
+    def drop_whole_turns(turns, name):
+        whole = consts.tile(list(turns.shape), F32, name=name)
+        nc.vector.tensor_scalar(out=whole[:], in0=turns, scalar1=ROUND, scalar2=ROUND, op0=ALU.add, op1=ALU.subtract)
+        sub(turns, turns, whole[:])
+
+    angles = consts.tile([P, LAYERS, PACK, 3], BF16)
+    bias = consts.tile([P, PACK], BF16)
+    with nc.allow_non_contiguous_dma(reason="a few bytes for each partition, once"):
+        nc.scalar.dma_start(out=angles[:], in_=params.rearrange("l (p t) a -> p l t a", t=PACK))
+        nc.scalar.dma_start(out=bias[:], in_=be3.rearrange("(p t) -> p t", t=PACK))
+
+    gate_turns = consts.tile([P, 2, LAYERS, PACK, 3], F32)
+    nc.vector.tensor_scalar(out=gate_turns[:, 0], in0=angles[:], scalar1=INV_TWO_PI, scalar2=None, op0=ALU.mult)
+    nc.vector.tensor_scalar(out=gate_turns[:, 1], in0=angles[:], scalar1=INV_TWO_PI, scalar2=0.25, op0=ALU.mult, op1=ALU.add)
+    drop_whole_turns(gate_turns[:], "gate_whole")
+    trig = consts.tile([P, 2, LAYERS, PACK, 3], F32)
+    nc.scalar.activation(out=trig[:], in_=gate_turns[:], func=ACT.Sin, scale=TWO_PI)
+
+    bias_turns = small("bias_turns")
+    nc.vector.tensor_scalar(out=bias_turns[:], in0=bias[:], scalar1=INV_TWO_PI, scalar2=None, op0=ALU.mult)
+
+    w = [small("w_x0"), small("w_y0"), small("w_z0")]
+    nc.vector.tensor_scalar(out=w[0][:], in0=trig[:, 0, 1, :, RY], scalar1=-1.0, scalar2=None, op0=ALU.mult)
+    nc.vector.memset(w[1][:], 0.0)
+    nc.vector.tensor_copy(out=w[2][:], in_=trig[:, 1, 1, :, RY])
+    step = 0
+    for layer, gate in ((1, RX), (0, RZ), (0, RY), (0, RX)):
+        step += 1
+        first, second = (gate + 1) % 3, (gate + 2) % 3
+        sin_g, cos_g = trig[:, 0, layer, :, gate], trig[:, 1, layer, :, gate]
+        fc, ss, sc, fs = [small("%s%d" % (n, step)) for n in ("fc", "ss", "sc", "fs")]
+        mul(fc[:], w[first][:], cos_g)
+        mul(ss[:], w[second][:], sin_g)
+        mul(sc[:], w[second][:], cos_g)
+        mul(fs[:], w[first][:], sin_g)
+        new_first, new_second = small("nf%d" % step), small("ns%d" % step)
+        add(new_first[:], fc[:], ss[:])
+        sub(new_second[:], sc[:], fs[:])
+        w[first], w[second] = new_first, new_second
+
+    sign = small("sign")
+    nc.vector.tensor_scalar(out=sign[:], in0=w[0][:], scalar1=0.0, scalar2=2.0, op0=ALU.is_ge, op1=ALU.mult)
+    nc.vector.tensor_scalar(out=sign[:], in0=sign[:], scalar1=-1.0, scalar2=None, op0=ALU.add)
+    xy = consts.tile([P, 2, PACK], F32)
+    yx = consts.tile([P, 2, PACK], F32)
+    mul(xy[:, 0, :], w[0][:], sign[:])
+    mul(xy[:, 1, :], w[2][:], sign[:])
+    nc.vector.tensor_copy(out=yx[:, 0, :], in_=xy[:, 1, :])
+    nc.vector.tensor_copy(out=yx[:, 1, :], in_=xy[:, 0, :])
+
+    size = small("size")
+    nc.vector.scalar_tensor_tensor(out=size[:], in0=xy[:, 1, :], scalar=-1.0, in1=xy[:, 1, :], op0=ALU.mult, op1=ALU.max)
+    nc.vector.scalar_tensor_tensor(out=size[:], in0=xy[:, 0, :], scalar=TINY, in1=size[:], op0=ALU.add, op1=ALU.add)
+    nc.vector.reciprocal(out=size[:], in_=size[:])
+    phase = small("phase")
+    nc.vector.scalar_tensor_tensor(out=phase[:], in0=xy[:, 1, :], scalar=HALF_PI, in1=size[:], op0=ALU.mult, op1=ALU.mult)
+
+    sin_cos = consts.tile([P, 2, PACK], F32)
+    cross = consts.tile([P, 2, PACK], F32)
+    dot = consts.tile([P, 2, PACK], F32)
+    along = small("along")
+    across = small("across")
+    for refinement in range(3):
+        nc.scalar.activation(out=sin_cos[:, 0, :], in_=phase[:], func=ACT.Sin)
+        nc.scalar.activation(out=sin_cos[:, 1, :], in_=phase[:], func=ACT.Sin, bias=HALF_PI)
+        mul(dot[:], sin_cos[:], yx[:])
+        nc.vector.scalar_tensor_tensor(out=along[:], in0=dot[:, 0, :], scalar=TINY, in1=dot[:, 1, :], op0=ALU.add, op1=ALU.add)
+        if refinement < 2:
+            mul(cross[:], sin_cos[:], xy[:])
+            sub(across[:], cross[:, 1, :], cross[:, 0, :])
+            nc.vector.reciprocal(out=along[:], in_=along[:])
+            mul(across[:], across[:], along[:])
+            add(phase[:], phase[:], across[:])
+
+    amplitude = small("amplitude")
+    mul(amplitude[:], along[:], sign[:])
+    phase_turns = small("phase_turns")
+    nc.vector.scalar_tensor_tensor(out=phase_turns[:], in0=phase[:], scalar=INV_TWO_PI, in1=bias_turns[:], op0=ALU.mult, op1=ALU.add)
+    drop_whole_turns(phase_turns[:], "phase_whole")
+    phase_rad = small("phase_rad")
+    nc.vector.tensor_scalar(out=phase_rad[:], in0=phase_turns[:], scalar1=TWO_PI, scalar2=None, op0=ALU.mult)
+    return amplitude, phase_turns, phase_rad
+
+
+def tile_unifiedautoencodernet_pa_t_kernel(tc, h_enc2, We3, be3, params, Wd1, bd1, out):
+    nc = tc.nc
+    with (
+        tc.tile_pool(name="consts", bufs=1) as consts,
+        tc.tile_pool(name="rows", bufs=4) as rows,
+        tc.tile_pool(name="stage", bufs=2) as stage,
+        tc.tile_pool(name="operands", bufs=3) as operands,
+        tc.tile_pool(name="planes", bufs=6) as planes,
+        tc.tile_pool(name="results", bufs=3) as results,
+        tc.psum_pool(name="psum_flip", bufs=2) as psum_flip,
+        tc.psum_pool(name="psum_theta", bufs=4) as psum_theta,
+        tc.psum_pool(name="psum_out", bufs=2) as psum_out,
+    ):
+        identity = consts.tile([P, P], F32)
+        make_identity(nc, identity[:])
+
+        we3_rows = consts.tile([P, PACK * WIDTH], BF16)
+        nc.sync.dma_start(out=we3_rows[:], in_=We3.rearrange("(m t) k -> m (t k)", t=PACK))
+        wd1_rows = consts.tile([P, BLOCKS * WIDTH], BF16)
+        bd1_rows = consts.tile([P, WIDTH], BF16)
+
+        amplitude, phase_turns, phase_rad = qubit_constants(nc, consts, params, be3)
+
+        we3_codes = consts.tile([P, WIDTH], U32, align_bytes=64)
+        we3_scales = consts.tile([P, WIDTH], U8, align_bytes=64)
+        we3_words = we3_rows[:].bitcast(F32)
+        transpose_and_quantise(
+            nc, psum_flip, stage, identity,
+            lambda n, u: we3_words[:, 256 * n + P * u : 256 * n + P * u + P],
+            we3_codes[:], we3_scales[:],
+        )
+
+        wd1_codes = consts.tile([P, WIDTH], U32, align_bytes=64)
+        wd1_scales = consts.tile([P, WIDTH], U8, align_bytes=64)
+
+        for c in range(CHUNKS):
+            chunk_rows = slice(c * CHUNK, (c + 1) * CHUNK)
+            h_rows = rows.tile([P, BLOCKS * WIDTH], BF16)
+            nc.sync.dma_start(out=h_rows[:], in_=h_enc2[chunk_rows, :].rearrange("(p r) k -> p (r k)", r=BLOCKS))
+            if c == 0:
+                nc.sync.dma_start(
+                    out=wd1_rows[:].rearrange("j (n q) -> j n q", n=BLOCKS), in_=Wd1.rearrange("(n j) q -> j n q", j=P)
+                )
+                nc.sync.dma_start(out=bd1_rows[:], in_=bd1.partition_broadcast(P))
+            h_words = h_rows[:].bitcast(F32)
+            h_codes = operands.tile([P, CHUNK], U32, align_bytes=64)
+            h_scales = operands.tile([P, CHUNK], U8, align_bytes=64)
+            transpose_and_quantise(
+                nc, psum_flip, stage, identity,
+                lambda n, u: h_words[:, 256 * n + P * u : 256 * n + P * u + P],
+                h_codes[:], h_scales[:],
+            )
+            if c == 0:
+                wd1_words = wd1_rows[:].bitcast(F32)
+                transpose_and_quantise(
+                    nc, psum_flip, stage, identity,
+                    lambda n, u: wd1_words[:, 256 * n + u : 256 * n + 256 : 2],
+                    wd1_codes[:], wd1_scales[:],
+                )
+
+            z_planes = stage.tile([P, PACK, CHUNK], BF16)
+            for t in range(PACK):
+                qubits = slice(t * P, (t + 1) * P)
+                theta = psum_theta.tile([P, CHUNK], F32)
+                nc.tensor.matmul_mx(
+                    out=theta[:],
+                    lhsT=we3_codes[:, qubits].bitcast(FP8X4), lhsT_scale=we3_scales[:, qubits],
+                    rhs=h_codes[:].bitcast(FP8X4), rhs_scale=h_scales[:],
+                    start=True, stop=True,
+                )
+                whole = planes.tile([P, CHUNK], I32)
+                nc.vector.tensor_scalar(
+                    out=whole[:], in0=theta[:], scalar1=INV_TWO_PI, scalar2=phase_turns[:, t : t + 1],
+                    op0=ALU.mult, op1=ALU.add,
+                )
+                part = planes.tile([P, CHUNK], F32)
+                nc.vector.scalar_tensor_tensor(
+                    out=part[:], in0=theta[:], scalar=INV_TWO_PI, in1=whole[:], op0=ALU.mult, op1=ALU.subtract
+                )
+                sine = planes.tile([P, CHUNK], F32)
+                nc.scalar.activation(out=sine[:], in_=part[:], func=ACT.Sin, scale=TWO_PI, bias=phase_rad[:, t : t + 1])
+                nc.gpsimd.tensor_scalar(
+                    out=z_planes[:, t, :], in0=sine[:], scalar1=amplitude[:, t : t + 1], scalar2=0.0,
+                    op0=ALU.mult, op1=ALU.add,
+                )
+            z_grouped = stage.tile([P, CHUNK * PACK], BF16, align_bytes=64)
+            nc.scalar.copy(
+                out=z_grouped[:].rearrange("p (b t) -> p b t", t=PACK), in_=z_planes[:].rearrange("p t b -> p b t")
+            )
+            z_codes = operands.tile([P, CHUNK], U32, align_bytes=64)
+            z_scales = operands.tile([P, CHUNK], U8, align_bytes=64)
+            nc.vector.quantize_mx(out=z_codes[:].bitcast(FP8X4), scales=z_scales[:], in_=z_grouped[:])
+
+            result = results.tile([P, BLOCKS, WIDTH], F32)
+            for r in range(BLOCKS):
+                block = slice(r * P, (r + 1) * P)
+                acc = psum_out.tile([P, WIDTH], F32)
+                nc.tensor.matmul_mx(
+                    out=acc[:],
+                    lhsT=z_codes[:, block].bitcast(FP8X4), lhsT_scale=z_scales[:, block],
+                    rhs=wd1_codes[:].bitcast(FP8X4), rhs_scale=wd1_scales[:],
+                    start=True, stop=True,
+                )
+                nc.vector.tensor_tensor(out=result[:, r, :], in0=acc[:], in1=bd1_rows[:], op=ALU.add)
+            nc.gpsimd.tensor_scalar(
+                out=result[:], in0=result[:], scalar1=FLT_MAX, scalar2=0.0, op0=ALU.min, op1=ALU.max
+            )
+            nc.sync.dma_start(out=out[chunk_rows, :].rearrange("(p r) j -> p r j", r=BLOCKS), in_=result[:])

@@ -32,19 +32,34 @@ FLT_MAX = 3.4028234663852886e38
 FLOPS = 2 * 2 * ROWS * WIDTH * WIDTH
 
 
-def transpose_and_quantise(nc, psum, stage, identity, word_block, codes, scales):
-    grouped = stage.tile([P, BLOCKS * P * PACK], BF16, align_bytes=64, tag="grouped")
-    grouped_words = grouped[:].bitcast(F32).rearrange("p (n c u) -> p n c u", n=BLOCKS, u=2)
+def transpose_words(nc, psum, identity, word_block):
+    banks = []
     for half in range(2):
-        flipped = psum.tile([P, 2, 2, P], F32, tag="flipped")
+        flipped = psum.tile([P, 2, 2, P], F32, tag="flipped", name="flipped")
         for n in range(2):
             for u in range(2):
                 nc.tensor.transpose(flipped[:, n, u, :], word_block(2 * half + n, u), identity[:])
-        nc.scalar.copy(
-            out=grouped_words[:, 2 * half : 2 * half + 2, :, :],
-            in_=flipped[:].rearrange("p n u c -> p n c u"),
-        )
-    nc.vector.quantize_mx(out=codes.bitcast(FP8X4), scales=scales, in_=grouped[:])
+        banks.append(flipped)
+    return banks
+
+
+def copy_out_grouped(nc, grouped, banks, half):
+    grouped_words = grouped[:].bitcast(F32).rearrange("p (n c u) -> p n c u", n=BLOCKS, u=2)
+    nc.scalar.copy(
+        out=grouped_words[:, 2 * half : 2 * half + 2, :, :],
+        in_=banks[half][:].rearrange("p n u c -> p n c u"),
+    )
+
+
+def quantise_weight(nc, psum, stage, consts, identity, word_block, name):
+    codes = consts.tile([P, WIDTH], U32, align_bytes=64, name=name + "_codes")
+    scales = consts.tile([P, WIDTH], U8, align_bytes=64, name=name + "_scales")
+    grouped = stage.tile([P, WIDTH * PACK], BF16, align_bytes=64, tag="grouped", name="grouped")
+    banks = transpose_words(nc, psum, identity, word_block)
+    for half in range(2):
+        copy_out_grouped(nc, grouped, banks, half)
+    nc.vector.quantize_mx(out=codes[:].bitcast(FP8X4), scales=scales[:], in_=grouped[:])
+    return codes, scales
 
 
 def qubit_constants(nc, consts, params, be3):
@@ -60,6 +75,9 @@ def qubit_constants(nc, consts, params, be3):
     def sub(out, a, b):
         nc.vector.tensor_tensor(out=out, in0=a, in1=b, op=ALU.subtract)
 
+    def repeated(values, times):
+        return values.unsqueeze(1).to_broadcast([P, times, PACK])
+
     def drop_whole_turns(turns, name):
         whole = consts.tile(list(turns.shape), F32, name=name)
         nc.vector.tensor_scalar(out=whole[:], in0=turns, scalar1=ROUND, scalar2=ROUND, op0=ALU.add, op1=ALU.subtract)
@@ -71,6 +89,10 @@ def qubit_constants(nc, consts, params, be3):
         nc.scalar.dma_start(out=angles[:], in_=params.rearrange("l (p t) a -> p l t a", t=PACK))
         nc.scalar.dma_start(out=bias[:], in_=be3.rearrange("(p t) -> p t", t=PACK))
 
+    warm = small("warm")
+    nc.vector.memset(warm[:], 0.0)
+    nc.scalar.activation(out=warm[:], in_=warm[:], func=ACT.Sin)
+
     gate_turns = consts.tile([P, 2, LAYERS, PACK, 3], F32)
     nc.vector.tensor_scalar(out=gate_turns[:, 0], in0=angles[:], scalar1=INV_TWO_PI, scalar2=None, op0=ALU.mult)
     nc.vector.tensor_scalar(out=gate_turns[:, 1], in0=angles[:], scalar1=INV_TWO_PI, scalar2=0.25, op0=ALU.mult, op1=ALU.add)
@@ -81,32 +103,25 @@ def qubit_constants(nc, consts, params, be3):
     bias_turns = small("bias_turns")
     nc.vector.tensor_scalar(out=bias_turns[:], in0=bias[:], scalar1=INV_TWO_PI, scalar2=None, op0=ALU.mult)
 
-    w = [small("w_x0"), small("w_y0"), small("w_z0")]
-    nc.vector.tensor_scalar(out=w[0][:], in0=trig[:, 0, 1, :, RY], scalar1=-1.0, scalar2=None, op0=ALU.mult)
-    nc.vector.memset(w[1][:], 0.0)
-    nc.vector.tensor_copy(out=w[2][:], in_=trig[:, 1, 1, :, RY])
-    step = 0
+    w = consts.tile([P, 3, PACK], F32)
+    nc.vector.tensor_scalar(out=w[:, 0, :], in0=trig[:, 0, 1, :, RY], scalar1=-1.0, scalar2=None, op0=ALU.mult)
+    nc.vector.memset(w[:, 1, :], 0.0)
+    nc.vector.tensor_copy(out=w[:, 2, :], in_=trig[:, 1, 1, :, RY])
     for layer, gate in ((1, RX), (0, RZ), (0, RY), (0, RX)):
-        step += 1
         first, second = (gate + 1) % 3, (gate + 2) % 3
-        sin_g, cos_g = trig[:, 0, layer, :, gate], trig[:, 1, layer, :, gate]
-        fc, ss, sc, fs = [small("%s%d" % (n, step)) for n in ("fc", "ss", "sc", "fs")]
-        mul(fc[:], w[first][:], cos_g)
-        mul(ss[:], w[second][:], sin_g)
-        mul(sc[:], w[second][:], cos_g)
-        mul(fs[:], w[first][:], sin_g)
-        new_first, new_second = small("nf%d" % step), small("ns%d" % step)
-        add(new_first[:], fc[:], ss[:])
-        sub(new_second[:], sc[:], fs[:])
-        w[first], w[second] = new_first, new_second
+        by_cos = consts.tile([P, 3, PACK], F32, name="by_cos_%d%d" % (layer, gate))
+        by_sin = consts.tile([P, 3, PACK], F32, name="by_sin_%d%d" % (layer, gate))
+        mul(by_cos[:], w[:], repeated(trig[:, 1, layer, :, gate], 3))
+        mul(by_sin[:], w[:], repeated(trig[:, 0, layer, :, gate], 3))
+        add(w[:, first, :], by_cos[:, first, :], by_sin[:, second, :])
+        sub(w[:, second, :], by_cos[:, second, :], by_sin[:, first, :])
 
     sign = small("sign")
-    nc.vector.tensor_scalar(out=sign[:], in0=w[0][:], scalar1=0.0, scalar2=2.0, op0=ALU.is_ge, op1=ALU.mult)
+    nc.vector.tensor_scalar(out=sign[:], in0=w[:, 0, :], scalar1=0.0, scalar2=2.0, op0=ALU.is_ge, op1=ALU.mult)
     nc.vector.tensor_scalar(out=sign[:], in0=sign[:], scalar1=-1.0, scalar2=None, op0=ALU.add)
     xy = consts.tile([P, 2, PACK], F32)
     yx = consts.tile([P, 2, PACK], F32)
-    mul(xy[:, 0, :], w[0][:], sign[:])
-    mul(xy[:, 1, :], w[2][:], sign[:])
+    mul(xy[:], w[:, 0:3:2, :], repeated(sign[:], 2))
     nc.vector.tensor_copy(out=yx[:, 0, :], in_=xy[:, 1, :])
     nc.vector.tensor_copy(out=yx[:, 1, :], in_=xy[:, 0, :])
 
@@ -114,8 +129,11 @@ def qubit_constants(nc, consts, params, be3):
     nc.vector.scalar_tensor_tensor(out=size[:], in0=xy[:, 1, :], scalar=-1.0, in1=xy[:, 1, :], op0=ALU.mult, op1=ALU.max)
     nc.vector.scalar_tensor_tensor(out=size[:], in0=xy[:, 0, :], scalar=TINY, in1=size[:], op0=ALU.add, op1=ALU.add)
     nc.vector.reciprocal(out=size[:], in_=size[:])
-    phase = small("phase")
-    nc.vector.scalar_tensor_tensor(out=phase[:], in0=xy[:, 1, :], scalar=HALF_PI, in1=size[:], op0=ALU.mult, op1=ALU.mult)
+    angle_pair = consts.tile([P, 2, PACK], F32)
+    nc.vector.scalar_tensor_tensor(
+        out=angle_pair[:, 0, :], in0=xy[:, 1, :], scalar=HALF_PI, in1=size[:], op0=ALU.mult, op1=ALU.mult
+    )
+    nc.vector.tensor_scalar(out=angle_pair[:, 1, :], in0=angle_pair[:, 0, :], scalar1=HALF_PI, scalar2=None, op0=ALU.add)
 
     sin_cos = consts.tile([P, 2, PACK], F32)
     cross = consts.tile([P, 2, PACK], F32)
@@ -123,8 +141,7 @@ def qubit_constants(nc, consts, params, be3):
     along = small("along")
     across = small("across")
     for refinement in range(3):
-        nc.scalar.activation(out=sin_cos[:, 0, :], in_=phase[:], func=ACT.Sin)
-        nc.scalar.activation(out=sin_cos[:, 1, :], in_=phase[:], func=ACT.Sin, bias=HALF_PI)
+        nc.scalar.activation(out=sin_cos[:], in_=angle_pair[:], func=ACT.Sin)
         mul(dot[:], sin_cos[:], yx[:])
         nc.vector.scalar_tensor_tensor(out=along[:], in0=dot[:, 0, :], scalar=TINY, in1=dot[:, 1, :], op0=ALU.add, op1=ALU.add)
         if refinement < 2:
@@ -132,12 +149,14 @@ def qubit_constants(nc, consts, params, be3):
             sub(across[:], cross[:, 1, :], cross[:, 0, :])
             nc.vector.reciprocal(out=along[:], in_=along[:])
             mul(across[:], across[:], along[:])
-            add(phase[:], phase[:], across[:])
+            add(angle_pair[:], angle_pair[:], repeated(across[:], 2))
 
     amplitude = small("amplitude")
     mul(amplitude[:], along[:], sign[:])
     phase_turns = small("phase_turns")
-    nc.vector.scalar_tensor_tensor(out=phase_turns[:], in0=phase[:], scalar=INV_TWO_PI, in1=bias_turns[:], op0=ALU.mult, op1=ALU.add)
+    nc.vector.scalar_tensor_tensor(
+        out=phase_turns[:], in0=angle_pair[:, 0, :], scalar=INV_TWO_PI, in1=bias_turns[:], op0=ALU.mult, op1=ALU.add
+    )
     drop_whole_turns(phase_turns[:], "phase_whole")
     phase_rad = small("phase_rad")
     nc.vector.tensor_scalar(out=phase_rad[:], in0=phase_turns[:], scalar1=TWO_PI, scalar2=None, op0=ALU.mult)
@@ -148,107 +167,173 @@ def tile_unifiedautoencodernet_pa_t_kernel(tc, h_enc2, We3, be3, params, Wd1, bd
     nc = tc.nc
     with (
         tc.tile_pool(name="consts", bufs=1) as consts,
-        tc.tile_pool(name="rows", bufs=4) as rows,
         tc.tile_pool(name="stage", bufs=2) as stage,
-        tc.tile_pool(name="operands", bufs=3) as operands,
-        tc.tile_pool(name="planes", bufs=6) as planes,
+        tc.tile_pool(name="planes", bufs=4) as planes,
         tc.tile_pool(name="results", bufs=3) as results,
         tc.psum_pool(name="psum_flip", bufs=2) as psum_flip,
         tc.psum_pool(name="psum_theta", bufs=4) as psum_theta,
         tc.psum_pool(name="psum_out", bufs=2) as psum_out,
     ):
-        identity = consts.tile([P, P], F32)
-        make_identity(nc, identity[:])
-
         we3_rows = consts.tile([P, PACK * WIDTH], BF16)
-        nc.sync.dma_start(out=we3_rows[:], in_=We3.rearrange("(m t) k -> m (t k)", t=PACK))
         wd1_rows = consts.tile([P, BLOCKS * WIDTH], BF16)
         bd1_rows = consts.tile([P, WIDTH], BF16)
-
-        amplitude, phase_turns, phase_rad = qubit_constants(nc, consts, params, be3)
-
-        we3_codes = consts.tile([P, WIDTH], U32, align_bytes=64)
-        we3_scales = consts.tile([P, WIDTH], U8, align_bytes=64)
-        we3_words = we3_rows[:].bitcast(F32)
-        transpose_and_quantise(
-            nc, psum_flip, stage, identity,
-            lambda n, u: we3_words[:, 256 * n + P * u : 256 * n + P * u + P],
-            we3_codes[:], we3_scales[:],
-        )
-
-        wd1_codes = consts.tile([P, WIDTH], U32, align_bytes=64)
-        wd1_scales = consts.tile([P, WIDTH], U8, align_bytes=64)
-
+        h_rows = [consts.tile([P, BLOCKS * WIDTH], BF16, name="h_rows_%d" % c) for c in range(CHUNKS)]
+        nc.sync.dma_start(out=we3_rows[:], in_=We3.rearrange("(m t) k -> m (t k)", t=PACK))
         for c in range(CHUNKS):
-            chunk_rows = slice(c * CHUNK, (c + 1) * CHUNK)
-            h_rows = rows.tile([P, BLOCKS * WIDTH], BF16)
-            nc.sync.dma_start(out=h_rows[:], in_=h_enc2[chunk_rows, :].rearrange("(p r) k -> p (r k)", r=BLOCKS))
-            if c == 0:
+            nc.sync.dma_start(
+                out=h_rows[c][:],
+                in_=h_enc2[c * CHUNK : (c + 1) * CHUNK, :].rearrange("(p r) k -> p (r k)", r=BLOCKS),
+            )
+            if c == 1:
                 nc.sync.dma_start(
                     out=wd1_rows[:].rearrange("j (n q) -> j n q", n=BLOCKS), in_=Wd1.rearrange("(n j) q -> j n q", j=P)
                 )
                 nc.sync.dma_start(out=bd1_rows[:], in_=bd1.partition_broadcast(P))
-            h_words = h_rows[:].bitcast(F32)
-            h_codes = operands.tile([P, CHUNK], U32, align_bytes=64)
-            h_scales = operands.tile([P, CHUNK], U8, align_bytes=64)
-            transpose_and_quantise(
-                nc, psum_flip, stage, identity,
-                lambda n, u: h_words[:, 256 * n + P * u : 256 * n + P * u + P],
-                h_codes[:], h_scales[:],
-            )
-            if c == 0:
-                wd1_words = wd1_rows[:].bitcast(F32)
-                transpose_and_quantise(
-                    nc, psum_flip, stage, identity,
-                    lambda n, u: wd1_words[:, 256 * n + u : 256 * n + 256 : 2],
-                    wd1_codes[:], wd1_scales[:],
-                )
 
-            z_planes = stage.tile([P, PACK, CHUNK], BF16)
-            for t in range(PACK):
+        identity = consts.tile([P, P], F32)
+        make_identity(nc, identity[:])
+        amplitude, phase_turns, phase_rad = qubit_constants(nc, consts, params, be3)
+
+        we3_words = we3_rows[:].bitcast(F32)
+        we3_codes, we3_scales = quantise_weight(
+            nc, psum_flip, stage, consts, identity,
+            lambda n, u: we3_words[:, 256 * n + P * u : 256 * n + P * u + P], "we3",
+        )
+        wd1_words = wd1_rows[:].bitcast(F32)
+        wd1_codes, wd1_scales = quantise_weight(
+            nc, psum_flip, stage, consts, identity,
+            lambda n, u: wd1_words[:, 256 * n + u : 256 * n + 256 : 2], "wd1",
+        )
+
+        flipped, h_grouped, h_mx, theta, whole, z_planes, z_grouped, z_mx, acc, result = [{} for n in range(10)]
+
+        def exists(c):
+            return 0 <= c < CHUNKS
+
+        def transpose_chunk(c):
+            if exists(c):
+                h_words = h_rows[c][:].bitcast(F32)
+                flipped[c] = transpose_words(
+                    nc, psum_flip, identity, lambda n, u: h_words[:, 256 * n + P * u : 256 * n + P * u + P]
+                )
+                h_grouped[c] = stage.tile([P, CHUNK * PACK], BF16, align_bytes=64, tag="grouped", name="grouped")
+
+        def copy_out_chunk(c, half):
+            if exists(c):
+                copy_out_grouped(nc, h_grouped[c], flipped[c], half)
+
+        def quantise_chunk(c):
+            if exists(c):
+                codes = stage.tile([P, CHUNK], U32, align_bytes=64, name="h_codes")
+                scales = stage.tile([P, CHUNK], U8, align_bytes=64, name="h_scales")
+                nc.vector.quantize_mx(out=codes[:].bitcast(FP8X4), scales=scales[:], in_=h_grouped[c][:])
+                h_mx[c] = (codes, scales)
+
+        def first_product(c, t):
+            if exists(c):
+                codes, scales = h_mx[c]
                 qubits = slice(t * P, (t + 1) * P)
-                theta = psum_theta.tile([P, CHUNK], F32)
+                theta[c, t] = psum_theta.tile([P, CHUNK], F32, name="theta")
                 nc.tensor.matmul_mx(
-                    out=theta[:],
+                    out=theta[c, t][:],
                     lhsT=we3_codes[:, qubits].bitcast(FP8X4), lhsT_scale=we3_scales[:, qubits],
-                    rhs=h_codes[:].bitcast(FP8X4), rhs_scale=h_scales[:],
+                    rhs=codes[:].bitcast(FP8X4), rhs_scale=scales[:],
                     start=True, stop=True,
                 )
-                whole = planes.tile([P, CHUNK], I32)
+
+        def whole_turns(c, t):
+            if exists(c):
+                whole[c, t] = planes.tile([P, CHUNK], I32, name="whole")
                 nc.vector.tensor_scalar(
-                    out=whole[:], in0=theta[:], scalar1=INV_TWO_PI, scalar2=phase_turns[:, t : t + 1],
+                    out=whole[c, t][:], in0=theta[c, t][:], scalar1=INV_TWO_PI, scalar2=phase_turns[:, t : t + 1],
                     op0=ALU.mult, op1=ALU.add,
                 )
-                part = planes.tile([P, CHUNK], F32)
+
+        def circuit(c, t):
+            if exists(c):
+                if t == 0:
+                    z_planes[c] = stage.tile([P, PACK, CHUNK], BF16, name="z_planes")
+                part = planes.tile([P, CHUNK], F32, name="part")
                 nc.vector.scalar_tensor_tensor(
-                    out=part[:], in0=theta[:], scalar=INV_TWO_PI, in1=whole[:], op0=ALU.mult, op1=ALU.subtract
+                    out=part[:], in0=theta[c, t][:], scalar=INV_TWO_PI, in1=whole[c, t][:],
+                    op0=ALU.mult, op1=ALU.subtract,
                 )
-                sine = planes.tile([P, CHUNK], F32)
+                sine = planes.tile([P, CHUNK], F32, name="sine")
                 nc.scalar.activation(out=sine[:], in_=part[:], func=ACT.Sin, scale=TWO_PI, bias=phase_rad[:, t : t + 1])
                 nc.gpsimd.tensor_scalar(
-                    out=z_planes[:, t, :], in0=sine[:], scalar1=amplitude[:, t : t + 1], scalar2=0.0,
+                    out=z_planes[c][:, t, :], in0=sine[:], scalar1=amplitude[:, t : t + 1], scalar2=0.0,
                     op0=ALU.mult, op1=ALU.add,
                 )
-            z_grouped = stage.tile([P, CHUNK * PACK], BF16, align_bytes=64)
-            nc.scalar.copy(
-                out=z_grouped[:].rearrange("p (b t) -> p b t", t=PACK), in_=z_planes[:].rearrange("p t b -> p b t")
-            )
-            z_codes = operands.tile([P, CHUNK], U32, align_bytes=64)
-            z_scales = operands.tile([P, CHUNK], U8, align_bytes=64)
-            nc.vector.quantize_mx(out=z_codes[:].bitcast(FP8X4), scales=z_scales[:], in_=z_grouped[:])
 
-            result = results.tile([P, BLOCKS, WIDTH], F32)
-            for r in range(BLOCKS):
+        def regroup_z(c):
+            if exists(c):
+                z_grouped[c] = stage.tile([P, CHUNK * PACK], BF16, align_bytes=64, name="z_grouped")
+                nc.scalar.copy(
+                    out=z_grouped[c][:].rearrange("p (b t) -> p b t", t=PACK),
+                    in_=z_planes[c][:].rearrange("p t b -> p b t"),
+                )
+
+        def quantise_z(c):
+            if exists(c):
+                codes = stage.tile([P, CHUNK], U32, align_bytes=64, name="z_codes")
+                scales = stage.tile([P, CHUNK], U8, align_bytes=64, name="z_scales")
+                nc.vector.quantize_mx(out=codes[:].bitcast(FP8X4), scales=scales[:], in_=z_grouped[c][:])
+                z_mx[c] = (codes, scales)
+                result[c] = results.tile([P, BLOCKS, WIDTH], F32, name="result")
+
+        def second_product(c, r):
+            if exists(c):
+                codes, scales = z_mx[c]
                 block = slice(r * P, (r + 1) * P)
-                acc = psum_out.tile([P, WIDTH], F32)
+                acc[c, r] = psum_out.tile([P, WIDTH], F32, name="acc")
                 nc.tensor.matmul_mx(
-                    out=acc[:],
-                    lhsT=z_codes[:, block].bitcast(FP8X4), lhsT_scale=z_scales[:, block],
+                    out=acc[c, r][:],
+                    lhsT=codes[:, block].bitcast(FP8X4), lhsT_scale=scales[:, block],
                     rhs=wd1_codes[:].bitcast(FP8X4), rhs_scale=wd1_scales[:],
                     start=True, stop=True,
                 )
-                nc.vector.tensor_tensor(out=result[:, r, :], in0=acc[:], in1=bd1_rows[:], op=ALU.add)
-            nc.gpsimd.tensor_scalar(
-                out=result[:], in0=result[:], scalar1=FLT_MAX, scalar2=0.0, op0=ALU.min, op1=ALU.max
-            )
-            nc.sync.dma_start(out=out[chunk_rows, :].rearrange("(p r) j -> p r j", r=BLOCKS), in_=result[:])
+
+        def add_bias(c, r):
+            if exists(c):
+                nc.vector.tensor_tensor(out=result[c][:, r, :], in0=acc[c, r][:], in1=bd1_rows[:], op=ALU.add)
+
+        def relu_and_store(c, half):
+            if exists(c):
+                pair = slice(2 * half, 2 * half + 2)
+                nc.gpsimd.tensor_scalar(
+                    out=result[c][:, pair, :], in0=result[c][:, pair, :], scalar1=FLT_MAX, scalar2=0.0,
+                    op0=ALU.min, op1=ALU.max,
+                )
+                chunk_out = out[c * CHUNK : (c + 1) * CHUNK, :].rearrange("(p r) j -> p r j", r=BLOCKS)
+                nc.sync.dma_start(out=chunk_out[:, pair, :], in_=result[c][:, pair, :])
+
+        with tc.manual_schedule():
+            for i in range(-2, CHUNKS + 1):
+                transpose_chunk(i + 2)
+                whole_turns(i, 0)
+                whole_turns(i, 1)
+                circuit(i, 0)
+                quantise_chunk(i + 1)
+                first_product(i + 1, 0)
+                copy_out_chunk(i + 2, 0)
+                whole_turns(i, 2)
+                circuit(i, 1)
+                first_product(i + 1, 1)
+                copy_out_chunk(i + 2, 1)
+                quantise_z(i - 1)
+                second_product(i - 1, 0)
+                second_product(i - 1, 1)
+                whole_turns(i, 3)
+                circuit(i, 2)
+                first_product(i + 1, 2)
+                add_bias(i - 1, 0)
+                second_product(i - 1, 2)
+                circuit(i, 3)
+                first_product(i + 1, 3)
+                regroup_z(i)
+                add_bias(i - 1, 1)
+                second_product(i - 1, 3)
+                relu_and_store(i - 1, 0)
+                add_bias(i - 1, 2)
+                add_bias(i - 1, 3)
+                relu_and_store(i - 1, 1)

@@ -205,7 +205,7 @@ def tile_unifiedautoencodernet_pa_t_kernel(tc, h_enc2, We3, be3, params, Wd1, bd
             lambda n, u: wd1_words[:, 256 * n + u : 256 * n + 256 : 2], "wd1",
         )
 
-        flipped, h_grouped, h_mx, theta, whole, z_planes, z_grouped, z_mx, acc, result = [{} for n in range(10)]
+        flipped, h_grouped, h_mx, theta, whole, part, z_planes, z_grouped, z_mx, acc, result = [{} for n in range(11)]
 
         def exists(c):
             return 0 <= c < CHUNKS
@@ -216,10 +216,11 @@ def tile_unifiedautoencodernet_pa_t_kernel(tc, h_enc2, We3, be3, params, Wd1, bd
                 flipped[c] = transpose_words(
                     nc, psum_flip, identity, lambda n, u: h_words[:, 256 * n + P * u : 256 * n + P * u + P]
                 )
-                h_grouped[c] = stage.tile([P, CHUNK * PACK], BF16, align_bytes=64, tag="grouped", name="grouped")
 
         def copy_out_chunk(c, half):
             if exists(c):
+                if half == 0:
+                    h_grouped[c] = stage.tile([P, CHUNK * PACK], BF16, align_bytes=64, tag="grouped", name="grouped")
                 copy_out_grouped(nc, h_grouped[c], flipped[c], half)
 
         def quantise_chunk(c):
@@ -249,17 +250,22 @@ def tile_unifiedautoencodernet_pa_t_kernel(tc, h_enc2, We3, be3, params, Wd1, bd
                     op0=ALU.mult, op1=ALU.add,
                 )
 
-        def circuit(c, t):
+        def part_of_turn(c, t):
+            if exists(c):
+                part[c, t] = planes.tile([P, CHUNK], F32, name="part")
+                nc.vector.scalar_tensor_tensor(
+                    out=part[c, t][:], in0=theta[c, t][:], scalar=INV_TWO_PI, in1=whole[c, t][:],
+                    op0=ALU.mult, op1=ALU.subtract,
+                )
+
+        def sine_wave(c, t):
             if exists(c):
                 if t == 0:
                     z_planes[c] = stage.tile([P, PACK, CHUNK], BF16, name="z_planes")
-                part = planes.tile([P, CHUNK], F32, name="part")
-                nc.vector.scalar_tensor_tensor(
-                    out=part[:], in0=theta[c, t][:], scalar=INV_TWO_PI, in1=whole[c, t][:],
-                    op0=ALU.mult, op1=ALU.subtract,
-                )
                 sine = planes.tile([P, CHUNK], F32, name="sine")
-                nc.scalar.activation(out=sine[:], in_=part[:], func=ACT.Sin, scale=TWO_PI, bias=phase_rad[:, t : t + 1])
+                nc.scalar.activation(
+                    out=sine[:], in_=part[c, t][:], func=ACT.Sin, scale=TWO_PI, bias=phase_rad[:, t : t + 1]
+                )
                 nc.gpsimd.tensor_scalar(
                     out=z_planes[c][:, t, :], in0=sine[:], scalar1=amplitude[:, t : t + 1], scalar2=0.0,
                     op0=ALU.mult, op1=ALU.add,
@@ -269,8 +275,8 @@ def tile_unifiedautoencodernet_pa_t_kernel(tc, h_enc2, We3, be3, params, Wd1, bd
             if exists(c):
                 z_grouped[c] = stage.tile([P, CHUNK * PACK], BF16, align_bytes=64, name="z_grouped")
                 nc.scalar.copy(
-                    out=z_grouped[c][:].rearrange("p (b t) -> p b t", t=PACK),
-                    in_=z_planes[c][:].rearrange("p t b -> p b t"),
+                    out=z_grouped[c][:].rearrange("p (b i t) -> p b t i", i=4, t=PACK),
+                    in_=z_planes[c][:].rearrange("p t (b i) -> p b t i", i=4),
                 )
 
         def quantise_z(c):
@@ -308,32 +314,36 @@ def tile_unifiedautoencodernet_pa_t_kernel(tc, h_enc2, We3, be3, params, Wd1, bd
                 nc.sync.dma_start(out=chunk_out[:, pair, :], in_=result[c][:, pair, :])
 
         with tc.manual_schedule():
-            for i in range(-2, CHUNKS + 1):
-                transpose_chunk(i + 2)
+            for i in range(-3, CHUNKS + 2):
+                copy_out_chunk(i + 2, 0)
+                copy_out_chunk(i + 2, 1)
+                transpose_chunk(i + 3)
+                regroup_z(i - 1)
                 whole_turns(i, 0)
                 whole_turns(i, 1)
-                circuit(i, 0)
+                part_of_turn(i, 0)
+                add_bias(i - 2, 1)
+                second_product(i - 2, 3)
+                relu_and_store(i - 2, 0)
+                sine_wave(i, 0)
                 quantise_chunk(i + 1)
                 first_product(i + 1, 0)
-                copy_out_chunk(i + 2, 0)
                 whole_turns(i, 2)
-                circuit(i, 1)
+                part_of_turn(i, 1)
                 first_product(i + 1, 1)
-                copy_out_chunk(i + 2, 1)
+                sine_wave(i, 1)
+                add_bias(i - 2, 2)
                 quantise_z(i - 1)
                 second_product(i - 1, 0)
-                second_product(i - 1, 1)
                 whole_turns(i, 3)
-                circuit(i, 2)
+                part_of_turn(i, 2)
                 first_product(i + 1, 2)
+                sine_wave(i, 2)
+                add_bias(i - 2, 3)
+                second_product(i - 1, 1)
+                part_of_turn(i, 3)
+                first_product(i + 1, 3)
+                sine_wave(i, 3)
+                relu_and_store(i - 2, 1)
                 add_bias(i - 1, 0)
                 second_product(i - 1, 2)
-                circuit(i, 3)
-                first_product(i + 1, 3)
-                regroup_z(i)
-                add_bias(i - 1, 1)
-                second_product(i - 1, 3)
-                relu_and_store(i - 1, 0)
-                add_bias(i - 1, 2)
-                add_bias(i - 1, 3)
-                relu_and_store(i - 1, 1)

@@ -29,42 +29,17 @@ ROUND = 12582912.0
 TINY = 1e-30
 FLT_MAX = 3.4028234663852886e38
 
+GUESS = (1.0375891712, 0.3825653414, 3.8018101902, -6.0852806269, 2.4341122508)
+GPSIMD_PLANES = (2, 3)
+
+PIECES = [(c, 0, BLOCKS) for c in range(CHUNKS - 1)] + [(CHUNKS - 1, 0, 2), (CHUNKS - 1, 2, 1), (CHUNKS - 1, 3, 1)]
+
 FLOPS = 2 * 2 * ROWS * WIDTH * WIDTH
 
 
-def transpose_words(nc, psum, identity, word_block):
-    banks = []
-    for half in range(2):
-        flipped = psum.tile([P, 2, 2, P], F32, tag="flipped", name="flipped")
-        for n in range(2):
-            for u in range(2):
-                nc.tensor.transpose(flipped[:, n, u, :], word_block(2 * half + n, u), identity[:])
-        banks.append(flipped)
-    return banks
-
-
-def copy_out_grouped(nc, grouped, banks, half):
-    grouped_words = grouped[:].bitcast(F32).rearrange("p (n c u) -> p n c u", n=BLOCKS, u=2)
-    nc.scalar.copy(
-        out=grouped_words[:, 2 * half : 2 * half + 2, :, :],
-        in_=banks[half][:].rearrange("p n u c -> p n c u"),
-    )
-
-
-def quantise_weight(nc, psum, stage, consts, identity, word_block, name):
-    codes = consts.tile([P, WIDTH], U32, align_bytes=64, name=name + "_codes")
-    scales = consts.tile([P, WIDTH], U8, align_bytes=64, name=name + "_scales")
-    grouped = stage.tile([P, WIDTH * PACK], BF16, align_bytes=64, tag="grouped", name="grouped")
-    banks = transpose_words(nc, psum, identity, word_block)
-    for half in range(2):
-        copy_out_grouped(nc, grouped, banks, half)
-    nc.vector.quantize_mx(out=codes[:].bitcast(FP8X4), scales=scales[:], in_=grouped[:])
-    return codes, scales
-
-
-def qubit_constants(nc, consts, params, be3):
-    def small(name):
-        return consts.tile([P, PACK], F32, name=name)
+def qubit_constants(nc, consts, angles, bias, between):
+    def small(name, *dims):
+        return consts.tile([P, *dims, PACK], F32, name=name)
 
     def mul(out, a, b):
         nc.vector.tensor_tensor(out=out, in0=a, in1=b, op=ALU.mult)
@@ -75,91 +50,102 @@ def qubit_constants(nc, consts, params, be3):
     def sub(out, a, b):
         nc.vector.tensor_tensor(out=out, in0=a, in1=b, op=ALU.subtract)
 
-    def repeated(values, times):
-        return values.unsqueeze(1).to_broadcast([P, times, PACK])
+    def twice(values):
+        return values.unsqueeze(1).to_broadcast([P, 2, PACK])
 
-    def drop_whole_turns(turns, name):
-        whole = consts.tile(list(turns.shape), F32, name=name)
-        nc.vector.tensor_scalar(out=whole[:], in0=turns, scalar1=ROUND, scalar2=ROUND, op0=ALU.add, op1=ALU.subtract)
-        sub(turns, turns, whole[:])
-
-    angles = consts.tile([P, LAYERS, PACK, 3], BF16)
-    bias = consts.tile([P, PACK], BF16)
-    with nc.allow_non_contiguous_dma(reason="a few bytes for each partition, once"):
-        nc.scalar.dma_start(out=angles[:], in_=params.rearrange("l (p t) a -> p l t a", t=PACK))
-        nc.scalar.dma_start(out=bias[:], in_=be3.rearrange("(p t) -> p t", t=PACK))
-
-    warm = small("warm")
-    nc.vector.memset(warm[:], 0.0)
-    nc.scalar.activation(out=warm[:], in_=warm[:], func=ACT.Sin)
-
-    gate_turns = consts.tile([P, 2, LAYERS, PACK, 3], F32)
-    nc.vector.tensor_scalar(out=gate_turns[:, 0], in0=angles[:], scalar1=INV_TWO_PI, scalar2=None, op0=ALU.mult)
-    nc.vector.tensor_scalar(out=gate_turns[:, 1], in0=angles[:], scalar1=INV_TWO_PI, scalar2=0.25, op0=ALU.mult, op1=ALU.add)
-    drop_whole_turns(gate_turns[:], "gate_whole")
-    trig = consts.tile([P, 2, LAYERS, PACK, 3], F32)
-    nc.scalar.activation(out=trig[:], in_=gate_turns[:], func=ACT.Sin, scale=TWO_PI)
-
+    turns = consts.tile([P, 2, LAYERS, PACK, 3], F32, name="turns")
+    nearest = consts.tile([P, 2, LAYERS, PACK, 3], I32, name="nearest")
+    for quarter in range(2):
+        for target in (nearest, turns):
+            nc.vector.tensor_scalar(
+                out=target[:, quarter], in0=angles[:], scalar1=INV_TWO_PI, scalar2=0.25 * quarter, op0=ALU.mult, op1=ALU.add
+            )
     bias_turns = small("bias_turns")
     nc.vector.tensor_scalar(out=bias_turns[:], in0=bias[:], scalar1=INV_TWO_PI, scalar2=None, op0=ALU.mult)
+    sub(turns[:], turns[:], nearest[:])
+    trig = consts.tile([P, 2, LAYERS, PACK, 3], F32, name="trig")
+    nc.scalar.activation(out=trig[:], in_=turns[:], func=ACT.Sin, scale=TWO_PI)
+    between(0)
 
-    w = consts.tile([P, 3, PACK], F32)
-    nc.vector.tensor_scalar(out=w[:, 0, :], in0=trig[:, 0, 1, :, RY], scalar1=-1.0, scalar2=None, op0=ALU.mult)
-    nc.vector.memset(w[:, 1, :], 0.0)
-    nc.vector.tensor_copy(out=w[:, 2, :], in_=trig[:, 1, 1, :, RY])
-    for layer, gate in ((1, RX), (0, RZ), (0, RY), (0, RX)):
-        first, second = (gate + 1) % 3, (gate + 2) % 3
-        by_cos = consts.tile([P, 3, PACK], F32, name="by_cos_%d%d" % (layer, gate))
-        by_sin = consts.tile([P, 3, PACK], F32, name="by_sin_%d%d" % (layer, gate))
-        mul(by_cos[:], w[:], repeated(trig[:, 1, layer, :, gate], 3))
-        mul(by_sin[:], w[:], repeated(trig[:, 0, layer, :, gate], 3))
-        add(w[:, first, :], by_cos[:, first, :], by_sin[:, second, :])
-        sub(w[:, second, :], by_cos[:, second, :], by_sin[:, first, :])
+    def sin(layer, gate):
+        return trig[:, 0, layer, :, gate]
+
+    def cos(layer, gate):
+        return trig[:, 1, layer, :, gate]
+
+    def both(layer, gate):
+        return trig[:, :, layer, :, gate]
+
+    u_yz, by_ux, by_uy, cx_y = [small(name, 2) for name in ("u_yz", "by_ux", "by_uy", "cx_y")]
+    s_uz, cc_uz, p, q, c_p, cs_p, s_q, rest = [
+        small(name) for name in ("s_uz", "cc_uz", "p", "q", "c_p", "cs_p", "s_q", "rest")
+    ]
+    w = small("w", 2)
+    mul(u_yz[:], both(1, RX), twice(cos(1, RY)))
+    mul(by_ux[:], both(0, RZ), twice(sin(1, RY)))
+    mul(cx_y[:], both(0, RY), twice(cos(0, RX)))
+    mul(by_uy[:], both(0, RZ), twice(u_yz[:, 0, :]))
+    mul(s_uz[:], sin(0, RY), u_yz[:, 1, :])
+    mul(cc_uz[:], cx_y[:, 1, :], u_yz[:, 1, :])
+    sub(p[:], by_uy[:, 0, :], by_ux[:, 1, :])
+    add(q[:], by_uy[:, 1, :], by_ux[:, 0, :])
+    mul(c_p[:], cos(0, RY), p[:])
+    mul(cs_p[:], cx_y[:, 0, :], p[:])
+    mul(s_q[:], sin(0, RX), q[:])
+    sub(w[:, 0, :], c_p[:], s_uz[:])
+    sub(rest[:], cc_uz[:], s_q[:])
 
     sign = small("sign")
-    nc.vector.tensor_scalar(out=sign[:], in0=w[:, 0, :], scalar1=0.0, scalar2=2.0, op0=ALU.is_ge, op1=ALU.mult)
-    nc.vector.tensor_scalar(out=sign[:], in0=sign[:], scalar1=-1.0, scalar2=None, op0=ALU.add)
-    xy = consts.tile([P, 2, PACK], F32)
-    yx = consts.tile([P, 2, PACK], F32)
-    mul(xy[:], w[:, 0:3:2, :], repeated(sign[:], 2))
-    nc.vector.tensor_copy(out=yx[:, 0, :], in_=xy[:, 1, :])
-    nc.vector.tensor_copy(out=yx[:, 1, :], in_=xy[:, 0, :])
+    nc.vector.tensor_scalar(out=sign[:], in0=w[:, 0, :], scalar1=0.0, scalar2=0.5, op0=ALU.is_ge, op1=ALU.subtract)
+    add(w[:, 1, :], rest[:], cs_p[:])
+    between(1)
+    xy = small("xy", 2)
+    mul(xy[:], w[:], twice(sign[:]))
 
-    size = small("size")
+    size, total, share, ratio, poly = [small(name) for name in ("size", "total", "share", "ratio", "poly")]
     nc.vector.scalar_tensor_tensor(out=size[:], in0=xy[:, 1, :], scalar=-1.0, in1=xy[:, 1, :], op0=ALU.mult, op1=ALU.max)
-    nc.vector.scalar_tensor_tensor(out=size[:], in0=xy[:, 0, :], scalar=TINY, in1=size[:], op0=ALU.add, op1=ALU.add)
-    nc.vector.reciprocal(out=size[:], in_=size[:])
-    angle_pair = consts.tile([P, 2, PACK], F32)
+    nc.vector.scalar_tensor_tensor(out=total[:], in0=xy[:, 0, :], scalar=TINY, in1=size[:], op0=ALU.add, op1=ALU.add)
+    nc.vector.reciprocal(out=total[:], in_=total[:])
+    mul(share[:], size[:], total[:])
+    mul(ratio[:], xy[:, 1, :], total[:])
+    nc.vector.tensor_scalar(out=poly[:], in0=share[:], scalar1=GUESS[4], scalar2=GUESS[3], op0=ALU.mult, op1=ALU.add)
+    between(2)
+    mul(poly[:], poly[:], share[:])
+    for degree in (2, 1):
+        nc.vector.scalar_tensor_tensor(
+            out=poly[:], in0=poly[:], scalar=GUESS[degree], in1=share[:], op0=ALU.add, op1=ALU.mult
+        )
+    angle = small("angle", 3)
+    for copy in (0, 2):
+        nc.vector.scalar_tensor_tensor(
+            out=angle[:, copy, :], in0=poly[:], scalar=GUESS[0], in1=ratio[:], op0=ALU.add, op1=ALU.mult
+        )
+    nc.vector.tensor_scalar(out=angle[:, 1, :], in0=angle[:, 0, :], scalar1=HALF_PI, scalar2=None, op0=ALU.add)
+    sin_cos_sin = small("sin_cos_sin", 3)
+    nc.scalar.activation(out=sin_cos_sin[:], in_=angle[:], func=ACT.Sin)
+    between(3)
+    base_turns = small("base_turns")
     nc.vector.scalar_tensor_tensor(
-        out=angle_pair[:, 0, :], in0=xy[:, 1, :], scalar=HALF_PI, in1=size[:], op0=ALU.mult, op1=ALU.mult
+        out=base_turns[:], in0=angle[:, 0, :], scalar=INV_TWO_PI, in1=bias_turns[:], op0=ALU.mult, op1=ALU.add
     )
-    nc.vector.tensor_scalar(out=angle_pair[:, 1, :], in0=angle_pair[:, 0, :], scalar1=HALF_PI, scalar2=None, op0=ALU.add)
 
-    sin_cos = consts.tile([P, 2, PACK], F32)
-    cross = consts.tile([P, 2, PACK], F32)
-    dot = consts.tile([P, 2, PACK], F32)
-    along = small("along")
-    across = small("across")
-    for refinement in range(3):
-        nc.scalar.activation(out=sin_cos[:], in_=angle_pair[:], func=ACT.Sin)
-        mul(dot[:], sin_cos[:], yx[:])
-        nc.vector.scalar_tensor_tensor(out=along[:], in0=dot[:, 0, :], scalar=TINY, in1=dot[:, 1, :], op0=ALU.add, op1=ALU.add)
-        if refinement < 2:
-            mul(cross[:], sin_cos[:], xy[:])
-            sub(across[:], cross[:, 1, :], cross[:, 0, :])
-            nc.vector.reciprocal(out=along[:], in_=along[:])
-            mul(across[:], across[:], along[:])
-            add(angle_pair[:], angle_pair[:], repeated(across[:], 2))
-
-    amplitude = small("amplitude")
-    mul(amplitude[:], along[:], sign[:])
-    phase_turns = small("phase_turns")
+    dot, cross = small("dot", 2), small("cross", 2)
+    along, inverse, across, error = [small(name) for name in ("along", "inverse", "across", "error")]
+    mul(dot[:], sin_cos_sin[:, 1:3, :], xy[:])
+    mul(cross[:], sin_cos_sin[:, 0:2, :], xy[:])
+    nc.vector.scalar_tensor_tensor(out=along[:], in0=dot[:, 0, :], scalar=TINY, in1=dot[:, 1, :], op0=ALU.add, op1=ALU.add)
+    sub(across[:], cross[:, 1, :], cross[:, 0, :])
+    nc.vector.reciprocal(out=inverse[:], in_=along[:])
+    mul(error[:], across[:], inverse[:])
+    phase_turns, phase_rad, amplitude = small("phase_turns"), small("phase_rad"), small("amplitude")
     nc.vector.scalar_tensor_tensor(
-        out=phase_turns[:], in0=angle_pair[:, 0, :], scalar=INV_TWO_PI, in1=bias_turns[:], op0=ALU.mult, op1=ALU.add
+        out=phase_turns[:], in0=error[:], scalar=INV_TWO_PI, in1=base_turns[:], op0=ALU.mult, op1=ALU.add
     )
-    drop_whole_turns(phase_turns[:], "phase_whole")
-    phase_rad = small("phase_rad")
+    between(4)
     nc.vector.tensor_scalar(out=phase_rad[:], in0=phase_turns[:], scalar1=TWO_PI, scalar2=None, op0=ALU.mult)
+    nc.vector.scalar_tensor_tensor(out=across[:], in0=across[:], scalar=0.5, in1=error[:], op0=ALU.mult, op1=ALU.mult)
+    add(along[:], along[:], across[:])
+    nc.vector.scalar_tensor_tensor(out=amplitude[:], in0=along[:], scalar=4.0, in1=sign[:], op0=ALU.mult, op1=ALU.mult)
     return amplitude, phase_turns, phase_rad
 
 
@@ -173,10 +159,16 @@ def tile_unifiedautoencodernet_pa_t_kernel(tc, h_enc2, We3, be3, params, Wd1, bd
         tc.psum_pool(name="psum_flip", bufs=2) as psum_flip,
         tc.psum_pool(name="psum_theta", bufs=4) as psum_theta,
         tc.psum_pool(name="psum_out", bufs=2) as psum_out,
+        tc.manual_schedule(),
     ):
-        we3_rows = consts.tile([P, PACK * WIDTH], BF16)
-        wd1_rows = consts.tile([P, BLOCKS * WIDTH], BF16)
-        bd1_rows = consts.tile([P, WIDTH], BF16)
+        angles = consts.tile([P, LAYERS, PACK, 3], BF16, name="angles")
+        bias = consts.tile([P, PACK], BF16, name="bias")
+        with nc.allow_non_contiguous_dma(reason="a few bytes for each partition, once"):
+            nc.scalar.dma_start(out=angles[:], in_=params.rearrange("l (p t) a -> p l t a", t=PACK))
+            nc.scalar.dma_start(out=bias[:], in_=be3.rearrange("(p t) -> p t", t=PACK))
+        we3_rows = consts.tile([P, PACK * WIDTH], BF16, name="we3_rows")
+        wd1_rows = consts.tile([P, BLOCKS * WIDTH], BF16, name="wd1_rows")
+        bd1_rows = consts.tile([P, WIDTH], BF16, name="bd1_rows")
         h_rows = [consts.tile([P, BLOCKS * WIDTH], BF16, name="h_rows_%d" % c) for c in range(CHUNKS)]
         nc.sync.dma_start(out=we3_rows[:], in_=We3.rearrange("(m t) k -> m (t k)", t=PACK))
         for c in range(CHUNKS):
@@ -184,166 +176,219 @@ def tile_unifiedautoencodernet_pa_t_kernel(tc, h_enc2, We3, be3, params, Wd1, bd
                 out=h_rows[c][:],
                 in_=h_enc2[c * CHUNK : (c + 1) * CHUNK, :].rearrange("(p r) k -> p (r k)", r=BLOCKS),
             )
-            if c == 1:
+            if c == 2:
                 nc.sync.dma_start(
                     out=wd1_rows[:].rearrange("j (n q) -> j n q", n=BLOCKS), in_=Wd1.rearrange("(n j) q -> j n q", j=P)
                 )
                 nc.sync.dma_start(out=bd1_rows[:], in_=bd1.partition_broadcast(P))
 
-        identity = consts.tile([P, P], F32)
+        warm = consts.tile([P, 1], F32, name="warm")
+        nc.vector.memset(warm[:], 0.0)
+        nc.scalar.activation(out=warm[:], in_=warm[:], func=ACT.Sin)
+        identity = consts.tile([P, P], F32, name="identity")
         make_identity(nc, identity[:])
-        amplitude, phase_turns, phase_rad = qubit_constants(nc, consts, params, be3)
 
-        we3_words = we3_rows[:].bitcast(F32)
-        we3_codes, we3_scales = quantise_weight(
-            nc, psum_flip, stage, consts, identity,
-            lambda n, u: we3_words[:, 256 * n + P * u : 256 * n + P * u + P], "we3",
-        )
-        wd1_words = wd1_rows[:].bitcast(F32)
-        wd1_codes, wd1_scales = quantise_weight(
-            nc, psum_flip, stage, consts, identity,
-            lambda n, u: wd1_words[:, 256 * n + u : 256 * n + 256 : 2], "wd1",
-        )
+        flipped, grouped, codes_of, scales_of, theta, turns, whole, part, z_planes, z_grouped, acc, result = [
+            {} for n in range(12)
+        ]
 
-        flipped, h_grouped, h_mx, theta, whole, part, z_planes, z_grouped, z_mx, acc, result = [{} for n in range(11)]
+        def exists(i):
+            return 0 <= i < len(PIECES)
 
-        def exists(c):
-            return 0 <= c < CHUNKS
+        def rows_of(i):
+            return PIECES[i][2] * P
 
-        def transpose_chunk(c):
-            if exists(c):
-                h_words = h_rows[c][:].bitcast(F32)
-                flipped[c] = transpose_words(
-                    nc, psum_flip, identity, lambda n, u: h_words[:, 256 * n + P * u : 256 * n + P * u + P]
+        def flip(key, psum, tag, blocks, word_block):
+            flipped[key] = []
+            for first in range(0, blocks, 2):
+                count = min(2, blocks - first)
+                bank = psum.tile([P, count, 2, P], F32, tag=tag, name=tag)
+                for n in range(count):
+                    for u in range(2):
+                        nc.tensor.transpose(bank[:, n, u, :], word_block(first + n, u), identity[:])
+                flipped[key].append(bank)
+
+        def copy_out(key, half):
+            banks = flipped[key]
+            count = banks[0][:].shape[1]
+            if half == 0:
+                width = count * len(banks) * P
+                grouped[key] = stage.tile([P, width * PACK], BF16, align_bytes=64, tag="grouped%d" % width, name="grouped")
+            words = grouped[key][:].bitcast(F32).rearrange("p (n c u) -> p n c u", c=P, u=2)
+            nc.scalar.copy(
+                out=words[:, count * half : count * (half + 1), :, :], in_=banks[half][:].rearrange("p n u c -> p n c u")
+            )
+
+        def quantise(key, source, pool, name):
+            width = source[:].shape[1] // PACK
+            codes = pool.tile([P, width], U32, align_bytes=64, name="%s_codes%d" % (name, width))
+            scales = pool.tile([P, width], U8, align_bytes=64, name="%s_scales%d" % (name, width))
+            nc.vector.quantize_mx(out=codes[:].bitcast(FP8X4), scales=scales[:], in_=source[:])
+            codes_of[key], scales_of[key] = codes, scales
+
+        def product(sums, left, left_columns, right):
+            nc.tensor.matmul_mx(
+                out=sums,
+                lhsT=codes_of[left][:, left_columns].bitcast(FP8X4), lhsT_scale=scales_of[left][:, left_columns],
+                rhs=codes_of[right][:].bitcast(FP8X4), rhs_scale=scales_of[right][:],
+                start=True, stop=True,
+            )
+
+        def flip_piece(i):
+            if exists(i):
+                chunk, first, blocks = PIECES[i]
+                words = h_rows[chunk][:].bitcast(F32)
+                flip(i, psum_flip, "flipped", blocks,
+                     lambda n, u: words[:, 256 * (first + n) + P * u : 256 * (first + n) + P * u + P])
+
+        def copy_out_piece(i):
+            if exists(i):
+                for half in range(len(flipped[i])):
+                    copy_out(i, half)
+
+        def quantise_piece(i):
+            if exists(i):
+                quantise(i, grouped[i], stage, "h")
+
+        def first_product(i, t):
+            if exists(i):
+                theta[i, t] = psum_theta.tile([P, rows_of(i)], F32, tag="theta", name="theta")
+                product(theta[i, t][:], "we3", slice(t * P, (t + 1) * P), i)
+
+        def turns_of(i, t):
+            if exists(i):
+                turns[i, t] = planes.tile([P, rows_of(i)], F32, tag="turns", name="turns_t")
+                nc.scalar.activation(
+                    out=turns[i, t][:], in_=theta[i, t][:], func=ACT.Identity, scale=INV_TWO_PI, bias=phase_turns[:, t : t + 1]
                 )
 
-        def copy_out_chunk(c, half):
-            if exists(c):
-                if half == 0:
-                    h_grouped[c] = stage.tile([P, CHUNK * PACK], BF16, align_bytes=64, tag="grouped", name="grouped")
-                copy_out_grouped(nc, h_grouped[c], flipped[c], half)
+        def whole_turns(i, t):
+            if exists(i):
+                if t in GPSIMD_PLANES:
+                    whole[i, t] = planes.tile([P, rows_of(i)], F32, tag="whole_f", name="whole_f")
+                    nc.gpsimd.tensor_scalar(
+                        out=whole[i, t][:], in0=turns[i, t][:], scalar1=ROUND, scalar2=ROUND, op0=ALU.add, op1=ALU.subtract
+                    )
+                else:
+                    whole[i, t] = planes.tile([P, rows_of(i)], I32, tag="whole", name="whole")
+                    nc.vector.tensor_scalar(
+                        out=whole[i, t][:], in0=theta[i, t][:], scalar1=INV_TWO_PI, scalar2=phase_turns[:, t : t + 1],
+                        op0=ALU.mult, op1=ALU.add,
+                    )
 
-        def quantise_chunk(c):
-            if exists(c):
-                codes = stage.tile([P, CHUNK], U32, align_bytes=64, name="h_codes")
-                scales = stage.tile([P, CHUNK], U8, align_bytes=64, name="h_scales")
-                nc.vector.quantize_mx(out=codes[:].bitcast(FP8X4), scales=scales[:], in_=h_grouped[c][:])
-                h_mx[c] = (codes, scales)
-
-        def first_product(c, t):
-            if exists(c):
-                codes, scales = h_mx[c]
-                qubits = slice(t * P, (t + 1) * P)
-                theta[c, t] = psum_theta.tile([P, CHUNK], F32, name="theta")
-                nc.tensor.matmul_mx(
-                    out=theta[c, t][:],
-                    lhsT=we3_codes[:, qubits].bitcast(FP8X4), lhsT_scale=we3_scales[:, qubits],
-                    rhs=codes[:].bitcast(FP8X4), rhs_scale=scales[:],
-                    start=True, stop=True,
-                )
-
-        def whole_turns(c, t):
-            if exists(c):
-                whole[c, t] = planes.tile([P, CHUNK], I32, name="whole")
-                nc.vector.tensor_scalar(
-                    out=whole[c, t][:], in0=theta[c, t][:], scalar1=INV_TWO_PI, scalar2=phase_turns[:, t : t + 1],
-                    op0=ALU.mult, op1=ALU.add,
-                )
-
-        def part_of_turn(c, t):
-            if exists(c):
-                part[c, t] = planes.tile([P, CHUNK], F32, name="part")
+        def part_of_turn(i, t):
+            if exists(i):
+                part[i, t] = planes.tile([P, rows_of(i)], F32, tag="part", name="part")
                 nc.vector.scalar_tensor_tensor(
-                    out=part[c, t][:], in0=theta[c, t][:], scalar=INV_TWO_PI, in1=whole[c, t][:],
+                    out=part[i, t][:], in0=theta[i, t][:], scalar=INV_TWO_PI, in1=whole[i, t][:],
                     op0=ALU.mult, op1=ALU.subtract,
                 )
 
-        def sine_wave(c, t):
-            if exists(c):
+        def sine_wave(i, t):
+            if exists(i):
                 if t == 0:
-                    z_planes[c] = stage.tile([P, PACK, CHUNK], BF16, name="z_planes")
-                sine = planes.tile([P, CHUNK], F32, name="sine")
+                    z_planes[i] = stage.tile([P, PACK, rows_of(i)], BF16, tag="z_planes%d" % rows_of(i), name="z_planes_i")
+                sine = planes.tile([P, rows_of(i)], F32, tag="sine", name="sine")
                 nc.scalar.activation(
-                    out=sine[:], in_=part[c, t][:], func=ACT.Sin, scale=TWO_PI, bias=phase_rad[:, t : t + 1]
+                    out=sine[:], in_=part[i, t][:], func=ACT.Sin, scale=TWO_PI, bias=phase_rad[:, t : t + 1]
                 )
                 nc.gpsimd.tensor_scalar(
-                    out=z_planes[c][:, t, :], in0=sine[:], scalar1=amplitude[:, t : t + 1], scalar2=0.0,
+                    out=z_planes[i][:, t, :], in0=sine[:], scalar1=amplitude[:, t : t + 1], scalar2=0.0,
                     op0=ALU.mult, op1=ALU.add,
                 )
 
-        def regroup_z(c):
-            if exists(c):
-                z_grouped[c] = stage.tile([P, CHUNK * PACK], BF16, align_bytes=64, name="z_grouped")
+        def regroup_z(i):
+            if exists(i):
+                width = rows_of(i) * PACK
+                z_grouped[i] = stage.tile([P, width], BF16, align_bytes=64, tag="z_grouped%d" % width, name="z_grouped_i")
                 nc.scalar.copy(
-                    out=z_grouped[c][:].rearrange("p (b i t) -> p b t i", i=4, t=PACK),
-                    in_=z_planes[c][:].rearrange("p t (b i) -> p b t i", i=4),
+                    out=z_grouped[i][:].rearrange("p (b i t) -> p b t i", i=4, t=PACK),
+                    in_=z_planes[i][:].rearrange("p t (b i) -> p b t i", i=4),
                 )
 
-        def quantise_z(c):
-            if exists(c):
-                codes = stage.tile([P, CHUNK], U32, align_bytes=64, name="z_codes")
-                scales = stage.tile([P, CHUNK], U8, align_bytes=64, name="z_scales")
-                nc.vector.quantize_mx(out=codes[:].bitcast(FP8X4), scales=scales[:], in_=z_grouped[c][:])
-                z_mx[c] = (codes, scales)
-                result[c] = results.tile([P, BLOCKS, WIDTH], F32, name="result")
+        def quantise_z(i):
+            if exists(i):
+                quantise(("z", i), z_grouped[i], stage, "z")
+                result[i] = results.tile([P, PIECES[i][2], WIDTH], F32, tag="result%d" % PIECES[i][2], name="result_i")
 
-        def second_product(c, r):
-            if exists(c):
-                codes, scales = z_mx[c]
-                block = slice(r * P, (r + 1) * P)
-                acc[c, r] = psum_out.tile([P, WIDTH], F32, name="acc")
-                nc.tensor.matmul_mx(
-                    out=acc[c, r][:],
-                    lhsT=codes[:, block].bitcast(FP8X4), lhsT_scale=scales[:, block],
-                    rhs=wd1_codes[:].bitcast(FP8X4), rhs_scale=wd1_scales[:],
-                    start=True, stop=True,
-                )
+        def second_product(i, r):
+            if exists(i) and r < PIECES[i][2]:
+                acc[i, r] = psum_out.tile([P, WIDTH], F32, tag="acc", name="acc")
+                product(acc[i, r][:], ("z", i), slice(r * P, (r + 1) * P), "wd1")
 
-        def add_bias(c, r):
-            if exists(c):
-                nc.vector.tensor_tensor(out=result[c][:, r, :], in0=acc[c, r][:], in1=bd1_rows[:], op=ALU.add)
+        def add_bias(i, r):
+            if exists(i) and r < PIECES[i][2]:
+                nc.vector.tensor_tensor(out=result[i][:, r, :], in0=acc[i, r][:], in1=bd1_rows[:], op=ALU.add)
 
-        def relu_and_store(c, half):
-            if exists(c):
-                pair = slice(2 * half, 2 * half + 2)
+        def relu_and_store(i, first, count):
+            if exists(i) and first < PIECES[i][2]:
+                chunk, start, blocks = PIECES[i]
+                pair = slice(first, min(first + count, blocks))
                 nc.gpsimd.tensor_scalar(
-                    out=result[c][:, pair, :], in0=result[c][:, pair, :], scalar1=FLT_MAX, scalar2=0.0,
+                    out=result[i][:, pair, :], in0=result[i][:, pair, :], scalar1=FLT_MAX, scalar2=0.0,
                     op0=ALU.min, op1=ALU.max,
                 )
-                chunk_out = out[c * CHUNK : (c + 1) * CHUNK, :].rearrange("(p r) j -> p r j", r=BLOCKS)
-                nc.sync.dma_start(out=chunk_out[:, pair, :], in_=result[c][:, pair, :])
+                chunk_out = out[chunk * CHUNK : (chunk + 1) * CHUNK, :].rearrange("(p r) j -> p r j", r=BLOCKS)
+                nc.sync.dma_start(out=chunk_out[:, start + pair.start : start + pair.stop, :], in_=result[i][:, pair, :])
 
-        with tc.manual_schedule():
-            for i in range(-3, CHUNKS + 2):
-                copy_out_chunk(i + 2, 0)
-                copy_out_chunk(i + 2, 1)
-                transpose_chunk(i + 3)
-                regroup_z(i - 1)
-                whole_turns(i, 0)
-                whole_turns(i, 1)
-                part_of_turn(i, 0)
-                add_bias(i - 2, 1)
-                second_product(i - 2, 3)
-                relu_and_store(i - 2, 0)
-                sine_wave(i, 0)
-                quantise_chunk(i + 1)
-                first_product(i + 1, 0)
-                whole_turns(i, 2)
-                part_of_turn(i, 1)
-                first_product(i + 1, 1)
-                sine_wave(i, 1)
-                add_bias(i - 2, 2)
-                quantise_z(i - 1)
-                second_product(i - 1, 0)
-                whole_turns(i, 3)
-                part_of_turn(i, 2)
-                first_product(i + 1, 2)
-                sine_wave(i, 2)
-                add_bias(i - 2, 3)
-                second_product(i - 1, 1)
-                part_of_turn(i, 3)
-                first_product(i + 1, 3)
-                sine_wave(i, 3)
-                relu_and_store(i - 2, 1)
-                add_bias(i - 1, 0)
-                second_product(i - 1, 2)
+        we3_words = we3_rows[:].bitcast(F32)
+        flip("we3", psum_out, "acc", BLOCKS, lambda n, u: we3_words[:, 256 * n + P * u : 256 * n + P * u + P])
+        wd1_words = wd1_rows[:].bitcast(F32)
+
+        def between(point):
+            if point == 0:
+                copy_out("we3", 0)
+                copy_out("we3", 1)
+                flip_piece(0)
+            if point == 1:
+                quantise("we3", grouped["we3"], consts, "we3")
+                copy_out_piece(0)
+                flip_piece(1)
+            if point == 2:
+                quantise_piece(0)
+                for t in range(PACK):
+                    first_product(0, t)
+            if point == 3:
+                copy_out_piece(1)
+
+        amplitude, phase_turns, phase_rad = qubit_constants(nc, consts, angles, bias, between)
+
+        for j in range(len(PIECES) + 2):
+            for t in GPSIMD_PLANES:
+                turns_of(j, t)
+            for t in GPSIMD_PLANES:
+                whole_turns(j, t)
+            regroup_z(j - 1)
+            quantise_piece(j + 1)
+            flip_piece(j + 2)
+            whole_turns(j, 0)
+            whole_turns(j, 1)
+            relu_and_store(j - 2, 2, 2)
+            part_of_turn(j, 0)
+            first_product(j + 1, 0)
+            sine_wave(j, 0)
+            part_of_turn(j, 1)
+            first_product(j + 1, 1)
+            sine_wave(j, 1)
+            part_of_turn(j, 2)
+            first_product(j + 1, 2)
+            sine_wave(j, 2)
+            quantise_z(j - 1)
+            second_product(j - 1, 0)
+            second_product(j - 1, 1)
+            part_of_turn(j, 3)
+            first_product(j + 1, 3)
+            sine_wave(j, 3)
+            add_bias(j - 1, 0)
+            second_product(j - 1, 2)
+            add_bias(j - 1, 1)
+            second_product(j - 1, 3)
+            relu_and_store(j - 1, 0, 2)
+            add_bias(j - 1, 2)
+            add_bias(j - 1, 3)
+            copy_out_piece(j + 2)
+            if j == 0:
+                flip("wd1", psum_out, "acc", BLOCKS, lambda n, u: wd1_words[:, 256 * n + u : 256 * n + 256 : 2])
+                copy_out("wd1", 0)
+                copy_out("wd1", 1)
+                quantise("wd1", grouped["wd1"], consts, "wd1")

@@ -25,12 +25,11 @@ RX, RY, RZ = 0, 1, 2
 TWO_PI = 2.0 * math.pi
 INV_TWO_PI = 1.0 / TWO_PI
 HALF_PI = 0.5 * math.pi
-ROUND = 12582912.0
 TINY = 1e-30
 FLT_MAX = 3.4028234663852886e38
 
 GUESS = (1.0375891712, 0.3825653414, 3.8018101902, -6.0852806269, 2.4341122508)
-GPSIMD_PLANES = (2, 3)
+TURNS_PLANES = (3,)
 
 PIECES = [(c, 0, BLOCKS) for c in range(CHUNKS - 1)] + [(CHUNKS - 1, 0, 2), (CHUNKS - 1, 2, 1), (CHUNKS - 1, 3, 1)]
 
@@ -264,10 +263,10 @@ def tile_unifiedautoencodernet_pa_t_kernel(tc, h_enc2, We3, be3, params, Wd1, bd
 
         def whole_turns(i, t):
             if exists(i):
-                if t in GPSIMD_PLANES:
-                    whole[i, t] = planes.tile([P, rows_of(i)], F32, tag="whole_f", name="whole_f")
+                if t in TURNS_PLANES:
+                    whole[i, t] = planes.tile([P, rows_of(i)], I32, tag="whole_g", name="whole_g")
                     nc.gpsimd.tensor_scalar(
-                        out=whole[i, t][:], in0=turns[i, t][:], scalar1=ROUND, scalar2=ROUND, op0=ALU.add, op1=ALU.subtract
+                        out=whole[i, t][:], in0=turns[i, t][:], scalar1=1.0, scalar2=0.0, op0=ALU.mult, op1=ALU.add
                     )
                 else:
                     whole[i, t] = planes.tile([P, rows_of(i)], I32, tag="whole", name="whole")
@@ -320,14 +319,21 @@ def tile_unifiedautoencodernet_pa_t_kernel(tc, h_enc2, We3, be3, params, Wd1, bd
             if exists(i) and r < PIECES[i][2]:
                 nc.vector.tensor_tensor(out=result[i][:, r, :], in0=acc[i, r][:], in1=bd1_rows[:], op=ALU.add)
 
-        def relu_and_store(i, first, count):
+        def relu_and_store(i, first, count, engine="gpsimd"):
             if exists(i) and first < PIECES[i][2]:
                 chunk, start, blocks = PIECES[i]
                 pair = slice(first, min(first + count, blocks))
-                nc.gpsimd.tensor_scalar(
-                    out=result[i][:, pair, :], in0=result[i][:, pair, :], scalar1=FLT_MAX, scalar2=0.0,
-                    op0=ALU.min, op1=ALU.max,
-                )
+                if engine == "scalar":
+                    nc.scalar.activation(out=result[i][:, pair, :], in_=result[i][:, pair, :], func=ACT.Relu)
+                elif engine == "vector":
+                    nc.vector.tensor_scalar(
+                        out=result[i][:, pair, :], in0=result[i][:, pair, :], scalar1=0.0, scalar2=None, op0=ALU.max
+                    )
+                else:
+                    nc.gpsimd.tensor_scalar(
+                        out=result[i][:, pair, :], in0=result[i][:, pair, :], scalar1=FLT_MAX, scalar2=0.0,
+                        op0=ALU.min, op1=ALU.max,
+                    )
                 chunk_out = out[chunk * CHUNK : (chunk + 1) * CHUNK, :].rearrange("(p r) j -> p r j", r=BLOCKS)
                 nc.sync.dma_start(out=chunk_out[:, start + pair.start : start + pair.stop, :], in_=result[i][:, pair, :])
 
@@ -343,51 +349,36 @@ def tile_unifiedautoencodernet_pa_t_kernel(tc, h_enc2, We3, be3, params, Wd1, bd
             if point == 1:
                 quantise("we3", grouped["we3"], consts, "we3")
                 copy_out_piece(0)
-                flip_piece(1)
             if point == 2:
                 quantise_piece(0)
-                for t in range(PACK):
-                    first_product(0, t)
-            if point == 3:
-                copy_out_piece(1)
 
         amplitude, phase_turns, phase_rad = qubit_constants(nc, consts, angles, bias, between)
 
-        for j in range(len(PIECES) + 2):
-            for t in GPSIMD_PLANES:
-                turns_of(j, t)
-            for t in GPSIMD_PLANES:
-                whole_turns(j, t)
-            regroup_z(j - 1)
-            quantise_piece(j + 1)
+        for j in range(-1, len(PIECES) + 2):
             flip_piece(j + 2)
-            whole_turns(j, 0)
-            whole_turns(j, 1)
-            relu_and_store(j - 2, 2, 2)
-            part_of_turn(j, 0)
-            first_product(j + 1, 0)
             sine_wave(j, 0)
-            part_of_turn(j, 1)
-            first_product(j + 1, 1)
-            sine_wave(j, 1)
-            part_of_turn(j, 2)
-            first_product(j + 1, 2)
-            sine_wave(j, 2)
+            first_product(j + 1, 0)
+            for t in (1, 3, 2):
+                part_of_turn(j, t)
+                sine_wave(j, t)
+                first_product(j + 1, t)
+            copy_out_piece(j + 2)
+            for r in range(BLOCKS):
+                add_bias(j - 2, r)
+                second_product(j - 2, r + 2)
+            for t in TURNS_PLANES:
+                turns_of(j + 1, t)
+            relu_and_store(j - 2, 0, 2)
+            relu_and_store(j - 2, 2, 2, "scalar")
+            for t in (3, 0, 1, 2):
+                whole_turns(j + 1, t)
+            part_of_turn(j + 1, 0)
+            regroup_z(j)
             quantise_z(j - 1)
             second_product(j - 1, 0)
             second_product(j - 1, 1)
-            part_of_turn(j, 3)
-            first_product(j + 1, 3)
-            sine_wave(j, 3)
-            add_bias(j - 1, 0)
-            second_product(j - 1, 2)
-            add_bias(j - 1, 1)
-            second_product(j - 1, 3)
-            relu_and_store(j - 1, 0, 2)
-            add_bias(j - 1, 2)
-            add_bias(j - 1, 3)
-            copy_out_piece(j + 2)
-            if j == 0:
+            quantise_piece(j + 2)
+            if j == -1:
                 flip("wd1", psum_out, "acc", BLOCKS, lambda n, u: wd1_words[:, 256 * n + u : 256 * n + 256 : 2])
                 copy_out("wd1", 0)
                 copy_out("wd1", 1)

@@ -31,7 +31,7 @@ FLT_MAX = 3.4028234663852886e38
 GUESS = (1.0375891712, 0.3825653414, 3.8018101902, -6.0852806269, 2.4341122508)
 TURNS_PLANES = (3,)
 
-PIECES = [(c, 0, BLOCKS) for c in range(CHUNKS - 1)] + [(CHUNKS - 1, 0, 2), (CHUNKS - 1, 2, 1), (CHUNKS - 1, 3, 1)]
+PIECES = [(c, 0, BLOCKS) for c in range(CHUNKS)]
 
 FLOPS = 2 * 2 * ROWS * WIDTH * WIDTH
 
@@ -98,28 +98,29 @@ def qubit_constants(nc, consts, angles, bias, between):
     nc.vector.tensor_scalar(out=sign[:], in0=w[:, 0, :], scalar1=0.0, scalar2=0.5, op0=ALU.is_ge, op1=ALU.subtract)
     add(w[:, 1, :], rest[:], cs_p[:])
     between(1)
-    xy = small("xy", 2)
-    mul(xy[:], w[:], twice(sign[:]))
 
-    size, total, share, ratio, poly = [small(name) for name in ("size", "total", "share", "ratio", "poly")]
-    nc.vector.scalar_tensor_tensor(out=size[:], in0=xy[:, 1, :], scalar=-1.0, in1=xy[:, 1, :], op0=ALU.mult, op1=ALU.max)
-    nc.vector.scalar_tensor_tensor(out=total[:], in0=xy[:, 0, :], scalar=TINY, in1=size[:], op0=ALU.add, op1=ALU.add)
+    xy, size = small("xy", 2), small("size", 2)
+    total, share, ratio, square, low, high, square_ratio = [
+        small(name) for name in ("total", "share", "ratio", "square", "low", "high", "square_ratio")
+    ]
+    nc.vector.scalar_tensor_tensor(out=size[:], in0=w[:], scalar=-1.0, in1=w[:], op0=ALU.mult, op1=ALU.max)
+    mul(xy[:], w[:], twice(sign[:]))
+    nc.vector.scalar_tensor_tensor(out=total[:], in0=size[:, 0, :], scalar=TINY, in1=size[:, 1, :], op0=ALU.add, op1=ALU.add)
     nc.vector.reciprocal(out=total[:], in_=total[:])
-    mul(share[:], size[:], total[:])
-    mul(ratio[:], xy[:, 1, :], total[:])
-    nc.vector.tensor_scalar(out=poly[:], in0=share[:], scalar1=GUESS[4], scalar2=GUESS[3], op0=ALU.mult, op1=ALU.add)
+    mul(share[:], size[:, 1, :], total[:])
+    nc.vector.scalar_tensor_tensor(out=ratio[:], in0=xy[:, 1, :], scalar=2.0, in1=total[:], op0=ALU.mult, op1=ALU.mult)
     between(2)
-    mul(poly[:], poly[:], share[:])
-    for degree in (2, 1):
-        nc.vector.scalar_tensor_tensor(
-            out=poly[:], in0=poly[:], scalar=GUESS[degree], in1=share[:], op0=ALU.add, op1=ALU.mult
-        )
+    mul(square[:], share[:], share[:])
+    nc.vector.tensor_scalar(out=high[:], in0=share[:], scalar1=GUESS[3], scalar2=GUESS[2], op0=ALU.mult, op1=ALU.add)
+    nc.vector.tensor_scalar(out=low[:], in0=share[:], scalar1=GUESS[1], scalar2=GUESS[0], op0=ALU.mult, op1=ALU.add)
+    nc.vector.scalar_tensor_tensor(out=high[:], in0=square[:], scalar=GUESS[4], in1=high[:], op0=ALU.mult, op1=ALU.add)
+    mul(square_ratio[:], square[:], ratio[:])
     angle = small("angle", 3)
-    for copy in (0, 2):
-        nc.vector.scalar_tensor_tensor(
-            out=angle[:, copy, :], in0=poly[:], scalar=GUESS[0], in1=ratio[:], op0=ALU.add, op1=ALU.mult
-        )
+    mul(angle[:, 0, :], low[:], ratio[:])
+    mul(angle[:, 2, :], low[:], ratio[:])
+    mul(high[:], high[:], square_ratio[:])
     nc.vector.tensor_scalar(out=angle[:, 1, :], in0=angle[:, 0, :], scalar1=HALF_PI, scalar2=None, op0=ALU.add)
+    add(angle[:], angle[:], high[:].unsqueeze(1).to_broadcast([P, 3, PACK]))
     sin_cos_sin = small("sin_cos_sin", 3)
     nc.scalar.activation(out=sin_cos_sin[:], in_=angle[:], func=ACT.Sin)
     between(3)
@@ -137,15 +138,22 @@ def qubit_constants(nc, consts, angles, bias, between):
     nc.vector.reciprocal(out=inverse[:], in_=along[:])
     mul(error[:], across[:], inverse[:])
     phase_turns, phase_rad, amplitude = small("phase_turns"), small("phase_rad"), small("amplitude")
+
+    def finish(step):
+        if step == 0:
+            nc.vector.tensor_scalar(out=phase_rad[:], in0=phase_turns[:], scalar1=TWO_PI, scalar2=None, op0=ALU.mult)
+            nc.vector.scalar_tensor_tensor(
+                out=across[:], in0=across[:], scalar=0.5, in1=error[:], op0=ALU.mult, op1=ALU.mult
+            )
+        if step == 1:
+            add(along[:], along[:], across[:])
+        if step == 2:
+            nc.vector.scalar_tensor_tensor(out=amplitude[:], in0=along[:], scalar=4.0, in1=sign[:], op0=ALU.mult, op1=ALU.mult)
+
     nc.vector.scalar_tensor_tensor(
         out=phase_turns[:], in0=error[:], scalar=INV_TWO_PI, in1=base_turns[:], op0=ALU.mult, op1=ALU.add
     )
-    between(4)
-    nc.vector.tensor_scalar(out=phase_rad[:], in0=phase_turns[:], scalar1=TWO_PI, scalar2=None, op0=ALU.mult)
-    nc.vector.scalar_tensor_tensor(out=across[:], in0=across[:], scalar=0.5, in1=error[:], op0=ALU.mult, op1=ALU.mult)
-    add(along[:], along[:], across[:])
-    nc.vector.scalar_tensor_tensor(out=amplitude[:], in0=along[:], scalar=4.0, in1=sign[:], op0=ALU.mult, op1=ALU.mult)
-    return amplitude, phase_turns, phase_rad
+    return amplitude, phase_turns, phase_rad, finish
 
 
 def tile_unifiedautoencodernet_pa_t_kernel(tc, h_enc2, We3, be3, params, Wd1, bd1, out):
@@ -154,7 +162,7 @@ def tile_unifiedautoencodernet_pa_t_kernel(tc, h_enc2, We3, be3, params, Wd1, bd
         tc.tile_pool(name="consts", bufs=1) as consts,
         tc.tile_pool(name="stage", bufs=2) as stage,
         tc.tile_pool(name="planes", bufs=4) as planes,
-        tc.tile_pool(name="results", bufs=3) as results,
+        tc.tile_pool(name="results", bufs=4) as results,
         tc.psum_pool(name="psum_flip", bufs=2) as psum_flip,
         tc.psum_pool(name="psum_theta", bufs=4) as psum_theta,
         tc.psum_pool(name="psum_out", bufs=2) as psum_out,
@@ -240,17 +248,16 @@ def tile_unifiedautoencodernet_pa_t_kernel(tc, h_enc2, We3, be3, params, Wd1, bd
                 flip(i, psum_flip, "flipped", blocks,
                      lambda n, u: words[:, 256 * (first + n) + P * u : 256 * (first + n) + P * u + P])
 
-        def copy_out_piece(i):
-            if exists(i):
-                for half in range(len(flipped[i])):
-                    copy_out(i, half)
+        def copy_out_piece(i, half):
+            if exists(i) and half < len(flipped[i]):
+                copy_out(i, half)
 
         def quantise_piece(i):
-            if exists(i):
+            if exists(i) and i not in codes_of:
                 quantise(i, grouped[i], stage, "h")
 
         def first_product(i, t):
-            if exists(i):
+            if exists(i) and (i, t) not in theta:
                 theta[i, t] = psum_theta.tile([P, rows_of(i)], F32, tag="theta", name="theta")
                 product(theta[i, t][:], "we3", slice(t * P, (t + 1) * P), i)
 
@@ -348,38 +355,58 @@ def tile_unifiedautoencodernet_pa_t_kernel(tc, h_enc2, We3, be3, params, Wd1, bd
                 flip_piece(0)
             if point == 1:
                 quantise("we3", grouped["we3"], consts, "we3")
-                copy_out_piece(0)
+                copy_out_piece(0, 0)
+                copy_out_piece(0, 1)
+                flip_piece(1)
             if point == 2:
                 quantise_piece(0)
+                for t in (3, 0, 1, 2):
+                    first_product(0, t)
 
-        amplitude, phase_turns, phase_rad = qubit_constants(nc, consts, angles, bias, between)
+        amplitude, phase_turns, phase_rad, finish_constants = qubit_constants(nc, consts, angles, bias, between)
 
         for j in range(-1, len(PIECES) + 2):
-            flip_piece(j + 2)
             sine_wave(j, 0)
-            first_product(j + 1, 0)
-            for t in (1, 3, 2):
-                part_of_turn(j, t)
-                sine_wave(j, t)
-                first_product(j + 1, t)
-            copy_out_piece(j + 2)
-            for r in range(BLOCKS):
-                add_bias(j - 2, r)
-                second_product(j - 2, r + 2)
-            for t in TURNS_PLANES:
-                turns_of(j + 1, t)
-            relu_and_store(j - 2, 0, 2)
-            relu_and_store(j - 2, 2, 2, "scalar")
-            for t in (3, 0, 1, 2):
-                whole_turns(j + 1, t)
-            part_of_turn(j + 1, 0)
-            regroup_z(j)
+            sine_wave(j, 1)
             quantise_z(j - 1)
             second_product(j - 1, 0)
             second_product(j - 1, 1)
-            quantise_piece(j + 2)
+            quantise_piece(j + 1)
+            copy_out_piece(j + 2, 0)
+            copy_out_piece(j + 2, 1)
+            part_of_turn(j, 3)
+            sine_wave(j, 3)
+            first_product(j + 1, 3)
+            part_of_turn(j, 2)
+            sine_wave(j, 2)
+            first_product(j + 1, 0)
+            add_bias(j - 1, 0)
+            second_product(j - 1, 2)
+            add_bias(j - 1, 1)
+            second_product(j - 1, 3)
+            first_product(j + 1, 1)
+            first_product(j + 1, 2)
+            turns_of(j + 1, 3)
+            whole_turns(j + 1, 3)
             if j == -1:
+                finish_constants(0)
+            whole_turns(j + 1, 0)
+            relu_and_store(j - 1, 0, 2, "scalar")
+            add_bias(j - 1, 2)
+            whole_turns(j + 1, 1)
+            if j == 0:
                 flip("wd1", psum_out, "acc", BLOCKS, lambda n, u: wd1_words[:, 256 * n + u : 256 * n + 256 : 2])
                 copy_out("wd1", 0)
                 copy_out("wd1", 1)
                 quantise("wd1", grouped["wd1"], consts, "wd1")
+            add_bias(j - 1, 3)
+            flip_piece(j + 3)
+            relu_and_store(j - 1, 2, 2)
+            part_of_turn(j + 1, 0)
+            part_of_turn(j + 1, 1)
+            if j == -1:
+                finish_constants(1)
+            whole_turns(j + 1, 2)
+            if j == -1:
+                finish_constants(2)
+            regroup_z(j)

@@ -195,8 +195,8 @@ def tile_unifiedautoencodernet_pa_t_kernel(tc, h_enc2, We3, be3, params, Wd1, bd
         identity = consts.tile([P, P], F32, name="identity")
         make_identity(nc, identity[:])
 
-        flipped, grouped, codes_of, scales_of, theta, turns, whole, part, z_planes, z_grouped, acc, result = [
-            {} for n in range(12)
+        flipped, grouped, codes_of, scales_of, theta, turns, whole, part, z_planes, z_grouped, acc, result, sines = [
+            {} for n in range(13)
         ]
 
         def exists(i):
@@ -298,28 +298,40 @@ def tile_unifiedautoencodernet_pa_t_kernel(tc, h_enc2, We3, be3, params, Wd1, bd
                 nc.scalar.activation(
                     out=sine[:], in_=part[i, t][:], func=ACT.Sin, scale=TWO_PI, bias=phase_rad[:, t : t + 1]
                 )
-                nc.gpsimd.tensor_scalar(
-                    out=z_planes[i][:, t, :], in0=sine[:], scalar1=amplitude[:, t : t + 1], scalar2=0.0,
+                sines[i, t] = sine
+
+        def multiply(i, t, engine=nc.gpsimd):
+            if exists(i):
+                engine.tensor_scalar(
+                    out=z_planes[i][:, t, :], in0=sines[i, t][:], scalar1=amplitude[:, t : t + 1], scalar2=0.0,
                     op0=ALU.mult, op1=ALU.add,
                 )
 
-        def regroup_z(i):
+        def regroup_z(i, first=0, count=BLOCKS, copy=nc.scalar.copy):
             if exists(i):
-                width = rows_of(i) * PACK
-                z_grouped[i] = stage.tile([P, width], BF16, align_bytes=64, tag="z_grouped%d" % width, name="z_grouped_i")
-                nc.scalar.copy(
-                    out=z_grouped[i][:].rearrange("p (b i t) -> p b t i", i=4, t=PACK),
-                    in_=z_planes[i][:].rearrange("p t (b i) -> p b t i", i=4),
+                if first == 0:
+                    z_grouped[i] = stage.tile([P, CHUNK * PACK], BF16, align_bytes=64, name="z_grouped_i")
+                rows = slice(first * P, (first + count) * P)
+                copy(
+                    out=z_grouped[i][:, PACK * rows.start : PACK * rows.stop].rearrange("p (b i t) -> p b t i", i=4, t=PACK),
+                    in_=z_planes[i][:, :, rows].rearrange("p t (b i) -> p b t i", i=4),
                 )
 
-        def quantise_z(i):
+        def quantise_z(i, first=0, count=BLOCKS):
             if exists(i):
-                quantise(("z", i), z_grouped[i], stage, "z")
-                result[i] = results.tile([P, PIECES[i][2], WIDTH], F32, tag="result%d" % PIECES[i][2], name="result_i")
+                if first == 0:
+                    codes_of["z", i] = stage.tile([P, CHUNK], U32, align_bytes=64, name="z_codes")
+                    scales_of["z", i] = stage.tile([P, CHUNK], U8, align_bytes=64, name="z_scales")
+                    result[i] = results.tile([P, BLOCKS, WIDTH], F32, name="result_i")
+                rows = slice(first * P, (first + count) * P)
+                nc.vector.quantize_mx(
+                    out=codes_of["z", i][:, rows].bitcast(FP8X4), scales=scales_of["z", i][:, rows],
+                    in_=z_grouped[i][:, PACK * rows.start : PACK * rows.stop],
+                )
 
-        def second_product(i, r):
+        def second_product(i, r, pool=psum_out, tag="acc"):
             if exists(i) and r < PIECES[i][2]:
-                acc[i, r] = psum_out.tile([P, WIDTH], F32, tag="acc", name="acc")
+                acc[i, r] = pool.tile([P, WIDTH], F32, tag=tag, name=tag)
                 product(acc[i, r][:], ("z", i), slice(r * P, (r + 1) * P), "wd1")
 
         def add_bias(i, r):
@@ -365,20 +377,26 @@ def tile_unifiedautoencodernet_pa_t_kernel(tc, h_enc2, We3, be3, params, Wd1, bd
 
         amplitude, phase_turns, phase_rad, finish_constants = qubit_constants(nc, consts, angles, bias, between)
 
-        for j in range(-1, len(PIECES) + 2):
+        for j in range(-1, CHUNKS - 1):
             sine_wave(j, 0)
+            multiply(j, 0)
             sine_wave(j, 1)
+            multiply(j, 1)
             quantise_z(j - 1)
             second_product(j - 1, 0)
             second_product(j - 1, 1)
             quantise_piece(j + 1)
             copy_out_piece(j + 2, 0)
             copy_out_piece(j + 2, 1)
+            if j == 0:
+                flip("wd1", psum_out, "acc", BLOCKS, lambda n, u: wd1_words[:, 256 * n + u : 256 * n + 256 : 2])
             part_of_turn(j, 3)
             sine_wave(j, 3)
+            multiply(j, 3)
             first_product(j + 1, 3)
             part_of_turn(j, 2)
             sine_wave(j, 2)
+            multiply(j, 2)
             first_product(j + 1, 0)
             add_bias(j - 1, 0)
             second_product(j - 1, 2)
@@ -386,19 +404,18 @@ def tile_unifiedautoencodernet_pa_t_kernel(tc, h_enc2, We3, be3, params, Wd1, bd
             second_product(j - 1, 3)
             first_product(j + 1, 1)
             first_product(j + 1, 2)
+            if j == 0:
+                copy_out("wd1", 0)
+                copy_out("wd1", 1)
             turns_of(j + 1, 3)
             whole_turns(j + 1, 3)
             if j == -1:
                 finish_constants(0)
             whole_turns(j + 1, 0)
-            relu_and_store(j - 1, 0, 2, "scalar")
+            relu_and_store(j - 1, 0, 1, "scalar")
+            relu_and_store(j - 1, 1, 1)
             add_bias(j - 1, 2)
             whole_turns(j + 1, 1)
-            if j == 0:
-                flip("wd1", psum_out, "acc", BLOCKS, lambda n, u: wd1_words[:, 256 * n + u : 256 * n + 256 : 2])
-                copy_out("wd1", 0)
-                copy_out("wd1", 1)
-                quantise("wd1", grouped["wd1"], consts, "wd1")
             add_bias(j - 1, 3)
             flip_piece(j + 3)
             relu_and_store(j - 1, 2, 2)
@@ -409,4 +426,41 @@ def tile_unifiedautoencodernet_pa_t_kernel(tc, h_enc2, We3, be3, params, Wd1, bd
             whole_turns(j + 1, 2)
             if j == -1:
                 finish_constants(2)
+            if j == 0:
+                quantise("wd1", grouped["wd1"], consts, "wd1")
             regroup_z(j)
+
+        last = CHUNKS - 1
+        for t in (0, 1):
+            sine_wave(last, t)
+            multiply(last, t)
+        quantise_z(last - 1)
+        second_product(last - 1, 0)
+        second_product(last - 1, 1)
+        part_of_turn(last, 3)
+        sine_wave(last, 3)
+        part_of_turn(last, 2)
+        sine_wave(last, 2)
+        add_bias(last - 1, 0)
+        second_product(last - 1, 2)
+        multiply(last, 3, nc.vector)
+        add_bias(last - 1, 1)
+        second_product(last - 1, 3)
+        relu_and_store(last - 1, 0, 2, "scalar")
+        multiply(last, 2, nc.vector)
+        add_bias(last - 1, 2)
+        for r in range(BLOCKS):
+            regroup_z(last, r, 1, nc.vector.tensor_copy)
+            if r == 1:
+                add_bias(last - 1, 3)
+                relu_and_store(last - 1, 2, 2, "scalar")
+            if r > 0:
+                quantise_z(last, r - 1, 1)
+                second_product(last, r - 1, psum_theta, "theta")
+        add_bias(last, 0)
+        relu_and_store(last, 0, 1)
+        quantise_z(last, 3, 1)
+        second_product(last, 3, psum_theta, "theta")
+        for r in range(1, BLOCKS):
+            add_bias(last, r)
+            relu_and_store(last, r, 1, "gpsimd" if r == 2 else "scalar")

@@ -412,8 +412,7 @@ def tile_unifiedautoencodernet_pa_t_kernel(tc, h_enc2, We3, be3, params, Wd1, bd
             if j == -1:
                 finish_constants(0)
             whole_turns(j + 1, 0)
-            relu_and_store(j - 1, 0, 1, "scalar")
-            relu_and_store(j - 1, 1, 1)
+            relu_and_store(j - 1, 0, 2, "scalar")
             add_bias(j - 1, 2)
             whole_turns(j + 1, 1)
             add_bias(j - 1, 3)

@@ -25,7 +25,7 @@ RX, RY, RZ = 0, 1, 2
 TWO_PI = 2.0 * math.pi
 INV_TWO_PI = 1.0 / TWO_PI
 HALF_PI = 0.5 * math.pi
-TINY = 1e-30
+TINY = 2.0**-100
 FLT_MAX = 3.4028234663852886e38
 
 GUESS = (1.0375891712, 0.3825653414, 3.8018101902, -6.0852806269, 2.4341122508)
@@ -36,7 +36,7 @@ PIECES = [(c, 0, BLOCKS) for c in range(CHUNKS)]
 FLOPS = 2 * 2 * ROWS * WIDTH * WIDTH
 
 
-def qubit_constants(nc, consts, angles, bias, between):
+def qubit_constants(nc, consts, angles, bias, quarter, w, between):
     def small(name, *dims):
         return consts.tile([P, *dims, PACK], F32, name=name)
 
@@ -52,19 +52,19 @@ def qubit_constants(nc, consts, angles, bias, between):
     def twice(values):
         return values.unsqueeze(1).to_broadcast([P, 2, PACK])
 
-    turns = consts.tile([P, 2, LAYERS, PACK, 3], F32, name="turns")
-    nearest = consts.tile([P, 2, LAYERS, PACK, 3], I32, name="nearest")
-    for quarter in range(2):
-        for target in (nearest, turns):
-            nc.vector.tensor_scalar(
-                out=target[:, quarter], in0=angles[:], scalar1=INV_TWO_PI, scalar2=0.25 * quarter, op0=ALU.mult, op1=ALU.add
-            )
-    bias_turns = small("bias_turns")
-    nc.vector.tensor_scalar(out=bias_turns[:], in0=bias[:], scalar1=INV_TWO_PI, scalar2=None, op0=ALU.mult)
+    gates = LAYERS * PACK * 3
+    turns = consts.tile([P, 2, gates], F32, name="turns")
+    nearest = consts.tile([P, 2, gates], I32, name="nearest")
+    for target in (nearest, turns):
+        nc.vector.scalar_tensor_tensor(
+            out=target[:], in0=angles[:].unsqueeze(1).to_broadcast([P, 2, gates]), scalar=INV_TWO_PI, in1=quarter[:],
+            op0=ALU.mult, op1=ALU.add,
+        )
     sub(turns[:], turns[:], nearest[:])
-    trig = consts.tile([P, 2, LAYERS, PACK, 3], F32, name="trig")
-    nc.scalar.activation(out=trig[:], in_=turns[:], func=ACT.Sin, scale=TWO_PI)
+    trig_flat = consts.tile([P, 2, gates], F32, name="trig")
+    nc.scalar.activation(out=trig_flat[:], in_=turns[:], func=ACT.Sin, scale=TWO_PI)
     between(0)
+    trig = trig_flat[:].rearrange("p s (l t g) -> p s l t g", l=LAYERS, t=PACK)
 
     def sin(layer, gate):
         return trig[:, 0, layer, :, gate]
@@ -76,55 +76,51 @@ def qubit_constants(nc, consts, angles, bias, between):
         return trig[:, :, layer, :, gate]
 
     u_yz, by_ux, by_uy, cx_y = [small(name, 2) for name in ("u_yz", "by_ux", "by_uy", "cx_y")]
-    s_uz, cc_uz, p, q, c_p, cs_p, s_q, rest = [
-        small(name) for name in ("s_uz", "cc_uz", "p", "q", "c_p", "cs_p", "s_q", "rest")
-    ]
-    w = small("w", 2)
+    s_uz, p, q, c_p = [small(name) for name in ("s_uz", "p", "q", "c_p")]
+    z_terms = consts.tile([P, PACK, 3], F32, name="z_terms")
     mul(u_yz[:], both(1, RX), twice(cos(1, RY)))
     mul(by_ux[:], both(0, RZ), twice(sin(1, RY)))
     mul(cx_y[:], both(0, RY), twice(cos(0, RX)))
     mul(by_uy[:], both(0, RZ), twice(u_yz[:, 0, :]))
     mul(s_uz[:], sin(0, RY), u_yz[:, 1, :])
-    mul(cc_uz[:], cx_y[:, 1, :], u_yz[:, 1, :])
+    mul(z_terms[:, :, 0], cx_y[:, 1, :], u_yz[:, 1, :])
     sub(p[:], by_uy[:, 0, :], by_ux[:, 1, :])
     add(q[:], by_uy[:, 1, :], by_ux[:, 0, :])
     mul(c_p[:], cos(0, RY), p[:])
-    mul(cs_p[:], cx_y[:, 0, :], p[:])
-    mul(s_q[:], sin(0, RX), q[:])
-    sub(w[:, 0, :], c_p[:], s_uz[:])
-    sub(rest[:], cc_uz[:], s_q[:])
+    mul(z_terms[:, :, 1], cx_y[:, 0, :], p[:])
+    nc.vector.scalar_tensor_tensor(out=z_terms[:, :, 2], in0=q[:], scalar=-1.0, in1=sin(0, RX), op0=ALU.mult, op1=ALU.mult)
+    sub(w[:, :, 0], c_p[:], s_uz[:])
+    nc.vector.tensor_reduce(out=w[:, :, 1], in_=z_terms[:], axis=mybir.AxisListType.X, op=ALU.add)
 
     sign = small("sign")
-    nc.vector.tensor_scalar(out=sign[:], in0=w[:, 0, :], scalar1=0.0, scalar2=0.5, op0=ALU.is_ge, op1=ALU.subtract)
-    add(w[:, 1, :], rest[:], cs_p[:])
-    between(1)
+    nc.vector.tensor_scalar(out=sign[:], in0=w[:, :, 0], scalar1=0.0, scalar2=0.5, op0=ALU.is_ge, op1=ALU.subtract)
 
-    xy, size = small("xy", 2), small("size", 2)
-    total, share, ratio, square, low, high, square_ratio = [
-        small(name) for name in ("total", "share", "ratio", "square", "low", "high", "square_ratio")
+    xy, total, share, ratio, square, low, high, square_ratio = [
+        small("xy", 2), *[small(name) for name in ("total", "share", "ratio", "square", "low", "high", "square_ratio")]
     ]
-    nc.vector.scalar_tensor_tensor(out=size[:], in0=w[:], scalar=-1.0, in1=w[:], op0=ALU.mult, op1=ALU.max)
-    mul(xy[:], w[:], twice(sign[:]))
-    nc.vector.scalar_tensor_tensor(out=total[:], in0=size[:, 0, :], scalar=TINY, in1=size[:, 1, :], op0=ALU.add, op1=ALU.add)
+    nc.vector.tensor_reduce(
+        out=total[:], in_=w[:], axis=mybir.AxisListType.X, op=ALU.add, apply_absolute_value=True
+    )
+    mul(xy[:], w[:, :, 0:2].rearrange("p t c -> p c t"), twice(sign[:]))
     nc.vector.reciprocal(out=total[:], in_=total[:])
-    mul(share[:], size[:, 1, :], total[:])
+    between(1)
     nc.vector.scalar_tensor_tensor(out=ratio[:], in0=xy[:, 1, :], scalar=2.0, in1=total[:], op0=ALU.mult, op1=ALU.mult)
-    between(2)
+    nc.vector.scalar_tensor_tensor(out=share[:], in0=ratio[:], scalar=-1.0, in1=ratio[:], op0=ALU.mult, op1=ALU.max)
     mul(square[:], share[:], share[:])
     nc.vector.tensor_scalar(out=high[:], in0=share[:], scalar1=GUESS[3], scalar2=GUESS[2], op0=ALU.mult, op1=ALU.add)
     nc.vector.tensor_scalar(out=low[:], in0=share[:], scalar1=GUESS[1], scalar2=GUESS[0], op0=ALU.mult, op1=ALU.add)
     nc.vector.scalar_tensor_tensor(out=high[:], in0=square[:], scalar=GUESS[4], in1=high[:], op0=ALU.mult, op1=ALU.add)
     mul(square_ratio[:], square[:], ratio[:])
     angle = small("angle", 3)
-    mul(angle[:, 0, :], low[:], ratio[:])
-    mul(angle[:, 2, :], low[:], ratio[:])
+    mul(angle[:, 0:3:2, :], twice(low[:]), twice(ratio[:]))
     mul(high[:], high[:], square_ratio[:])
     nc.vector.tensor_scalar(out=angle[:, 1, :], in0=angle[:, 0, :], scalar1=HALF_PI, scalar2=None, op0=ALU.add)
     add(angle[:], angle[:], high[:].unsqueeze(1).to_broadcast([P, 3, PACK]))
     sin_cos_sin = small("sin_cos_sin", 3)
     nc.scalar.activation(out=sin_cos_sin[:], in_=angle[:], func=ACT.Sin)
-    between(3)
-    base_turns = small("base_turns")
+    between(2)
+    bias_turns, base_turns = small("bias_turns"), small("base_turns")
+    nc.vector.tensor_scalar(out=bias_turns[:], in0=bias[:], scalar1=INV_TWO_PI, scalar2=None, op0=ALU.mult)
     nc.vector.scalar_tensor_tensor(
         out=base_turns[:], in0=angle[:, 0, :], scalar=INV_TWO_PI, in1=bias_turns[:], op0=ALU.mult, op1=ALU.add
     )
@@ -168,10 +164,13 @@ def tile_unifiedautoencodernet_pa_t_kernel(tc, h_enc2, We3, be3, params, Wd1, bd
         tc.psum_pool(name="psum_out", bufs=2) as psum_out,
         tc.manual_schedule(),
     ):
-        angles = consts.tile([P, LAYERS, PACK, 3], BF16, name="angles")
+        angles = consts.tile([P, LAYERS * PACK * 3], BF16, name="angles")
         bias = consts.tile([P, PACK], BF16, name="bias")
         with nc.allow_non_contiguous_dma(reason="a few bytes for each partition, once"):
-            nc.scalar.dma_start(out=angles[:], in_=params.rearrange("l (p t) a -> p l t a", t=PACK))
+            nc.sync.dma_start(
+                out=angles[:].rearrange("p (l t a) -> p l t a", l=LAYERS, t=PACK),
+                in_=params.rearrange("l (p t) a -> p l t a", t=PACK),
+            )
             nc.scalar.dma_start(out=bias[:], in_=be3.rearrange("(p t) -> p t", t=PACK))
         we3_rows = consts.tile([P, PACK * WIDTH], BF16, name="we3_rows")
         wd1_rows = consts.tile([P, BLOCKS * WIDTH], BF16, name="wd1_rows")
@@ -189,6 +188,11 @@ def tile_unifiedautoencodernet_pa_t_kernel(tc, h_enc2, We3, be3, params, Wd1, bd
                 )
                 nc.sync.dma_start(out=bd1_rows[:], in_=bd1.partition_broadcast(P))
 
+        quarter = consts.tile([P, 2, LAYERS * PACK * 3], F32, name="quarter")
+        nc.gpsimd.memset(quarter[:, 0, :], 0.0)
+        nc.gpsimd.memset(quarter[:, 1, :], 0.25)
+        w = consts.tile([P, PACK, 3], F32, name="w")
+        nc.vector.memset(w[:], TINY)
         warm = consts.tile([P, 1], F32, name="warm")
         nc.vector.memset(warm[:], 0.0)
         nc.scalar.activation(out=warm[:], in_=warm[:], func=ACT.Sin)
@@ -375,9 +379,10 @@ def tile_unifiedautoencodernet_pa_t_kernel(tc, h_enc2, We3, be3, params, Wd1, bd
                 for t in (3, 0, 1, 2):
                     first_product(0, t)
 
-        amplitude, phase_turns, phase_rad, finish_constants = qubit_constants(nc, consts, angles, bias, between)
+        amplitude, phase_turns, phase_rad, finish_constants = qubit_constants(nc, consts, angles, bias, quarter, w, between)
 
         for j in range(-1, CHUNKS - 1):
+            copy_out_piece(j + 2, 0)
             sine_wave(j, 0)
             multiply(j, 0)
             sine_wave(j, 1)
@@ -386,10 +391,9 @@ def tile_unifiedautoencodernet_pa_t_kernel(tc, h_enc2, We3, be3, params, Wd1, bd
             second_product(j - 1, 0)
             second_product(j - 1, 1)
             quantise_piece(j + 1)
-            copy_out_piece(j + 2, 0)
-            copy_out_piece(j + 2, 1)
             if j == 0:
                 flip("wd1", psum_out, "acc", BLOCKS, lambda n, u: wd1_words[:, 256 * n + u : 256 * n + 256 : 2])
+            copy_out_piece(j + 2, 1)
             part_of_turn(j, 3)
             sine_wave(j, 3)
             multiply(j, 3)

@@ -383,44 +383,43 @@ def tile_unifiedautoencodernet_pa_t_kernel(tc, h_enc2, We3, be3, params, Wd1, bd
 
         for j in range(-1, CHUNKS - 1):
             copy_out_piece(j + 2, 0)
-            sine_wave(j, 0)
-            multiply(j, 0)
-            sine_wave(j, 1)
-            multiply(j, 1)
+            for t in (0, 1):
+                sine_wave(j, t)
+                multiply(j, t)
             quantise_z(j - 1)
             second_product(j - 1, 0)
             second_product(j - 1, 1)
             quantise_piece(j + 1)
             if j == 0:
                 flip("wd1", psum_out, "acc", BLOCKS, lambda n, u: wd1_words[:, 256 * n + u : 256 * n + 256 : 2])
-            copy_out_piece(j + 2, 1)
-            part_of_turn(j, 3)
-            sine_wave(j, 3)
-            multiply(j, 3)
-            first_product(j + 1, 3)
-            part_of_turn(j, 2)
-            sine_wave(j, 2)
-            multiply(j, 2)
             first_product(j + 1, 0)
+            copy_out_piece(j + 2, 1)
+            for t in (3, 2):
+                part_of_turn(j, t)
+                sine_wave(j, t)
+                multiply(j, t)
+            first_product(j + 1, 3)
+            first_product(j + 1, 1)
             add_bias(j - 1, 0)
             second_product(j - 1, 2)
+            relu_and_store(j - 1, 0, 1, "scalar")
             add_bias(j - 1, 1)
             second_product(j - 1, 3)
-            first_product(j + 1, 1)
             first_product(j + 1, 2)
+            flip_piece(j + 3)
             if j == 0:
                 copy_out("wd1", 0)
-                copy_out("wd1", 1)
             turns_of(j + 1, 3)
             whole_turns(j + 1, 3)
+            if j == 0:
+                copy_out("wd1", 1)
+            relu_and_store(j - 1, 1, 1, "scalar")
             if j == -1:
                 finish_constants(0)
             whole_turns(j + 1, 0)
-            relu_and_store(j - 1, 0, 2, "scalar")
-            add_bias(j - 1, 2)
             whole_turns(j + 1, 1)
+            add_bias(j - 1, 2)
             add_bias(j - 1, 3)
-            flip_piece(j + 3)
             relu_and_store(j - 1, 2, 2)
             part_of_turn(j + 1, 0)
             part_of_turn(j + 1, 1)
@@ -440,30 +439,27 @@ def tile_unifiedautoencodernet_pa_t_kernel(tc, h_enc2, We3, be3, params, Wd1, bd
         quantise_z(last - 1)
         second_product(last - 1, 0)
         second_product(last - 1, 1)
-        part_of_turn(last, 3)
-        sine_wave(last, 3)
-        part_of_turn(last, 2)
-        sine_wave(last, 2)
+        for t in (3, 2):
+            part_of_turn(last, t)
+            sine_wave(last, t)
         add_bias(last - 1, 0)
         second_product(last - 1, 2)
         multiply(last, 3, nc.vector)
+        multiply(last, 2, nc.vector)
         add_bias(last - 1, 1)
         second_product(last - 1, 3)
-        relu_and_store(last - 1, 0, 2, "scalar")
-        multiply(last, 2, nc.vector)
+        relu_and_store(last - 1, 0, 2)
+        regroup_z(last, 0, 1)
+        regroup_z(last, 1, 1, nc.vector.tensor_copy)
+        regroup_z(last, 2, 1)
         add_bias(last - 1, 2)
+        add_bias(last - 1, 3)
+        relu_and_store(last - 1, 2, 2, "scalar")
         for r in range(BLOCKS):
-            regroup_z(last, r, 1, nc.vector.tensor_copy)
+            quantise_z(last, r, 1)
+            second_product(last, r, psum_theta, "theta")
             if r == 1:
-                add_bias(last - 1, 3)
-                relu_and_store(last - 1, 2, 2, "scalar")
-            if r > 0:
-                quantise_z(last, r - 1, 1)
-                second_product(last, r - 1, psum_theta, "theta")
-        add_bias(last, 0)
-        relu_and_store(last, 0, 1)
-        quantise_z(last, 3, 1)
-        second_product(last, 3, psum_theta, "theta")
-        for r in range(1, BLOCKS):
+                regroup_z(last, 3, 1, nc.vector.tensor_copy)
+        for r in range(BLOCKS):
             add_bias(last, r)
-            relu_and_store(last, r, 1, "gpsimd" if r == 2 else "scalar")
+            relu_and_store(last, r, 1, ("gpsimd", "scalar")[r % 2])

@@ -28,6 +28,7 @@ HALF_PI = 0.5 * math.pi
 TINY = 2.0**-100
 FLT_MAX = 3.4028234663852886e38
 
+RUN = 8
 GUESS = (1.0375891712, 0.3825653414, 3.8018101902, -6.0852806269, 2.4341122508)
 TURNS_PLANES = (3,)
 
@@ -95,22 +96,23 @@ def qubit_constants(nc, consts, angles, bias, quarter, w, between):
     sign = small("sign")
     nc.vector.tensor_scalar(out=sign[:], in0=w[:, :, 0], scalar1=0.0, scalar2=0.5, op0=ALU.is_ge, op1=ALU.subtract)
 
-    xy, total, share, ratio, square, low, high, square_ratio = [
-        small("xy", 2), *[small(name) for name in ("total", "share", "ratio", "square", "low", "high", "square_ratio")]
+    xy, size, total, share, ratio, square, low, high, square_ratio = [
+        small("xy", 2), *[small(name) for name in ("size", "total", "share", "ratio", "square", "low", "high", "square_ratio")]
     ]
     nc.vector.tensor_reduce(
         out=total[:], in_=w[:], axis=mybir.AxisListType.X, op=ALU.add, apply_absolute_value=True
     )
     mul(xy[:], w[:, :, 0:2].rearrange("p t c -> p c t"), twice(sign[:]))
+    nc.vector.scalar_tensor_tensor(out=size[:], in0=w[:, :, 1], scalar=-1.0, in1=w[:, :, 1], op0=ALU.mult, op1=ALU.max)
     nc.vector.reciprocal(out=total[:], in_=total[:])
-    between(1)
     nc.vector.scalar_tensor_tensor(out=ratio[:], in0=xy[:, 1, :], scalar=2.0, in1=total[:], op0=ALU.mult, op1=ALU.mult)
-    nc.vector.scalar_tensor_tensor(out=share[:], in0=ratio[:], scalar=-1.0, in1=ratio[:], op0=ALU.mult, op1=ALU.max)
+    mul(share[:], size[:], total[:])
     mul(square[:], share[:], share[:])
     nc.vector.tensor_scalar(out=high[:], in0=share[:], scalar1=GUESS[3], scalar2=GUESS[2], op0=ALU.mult, op1=ALU.add)
     nc.vector.tensor_scalar(out=low[:], in0=share[:], scalar1=GUESS[1], scalar2=GUESS[0], op0=ALU.mult, op1=ALU.add)
     nc.vector.scalar_tensor_tensor(out=high[:], in0=square[:], scalar=GUESS[4], in1=high[:], op0=ALU.mult, op1=ALU.add)
     mul(square_ratio[:], square[:], ratio[:])
+    between(1)
     angle = small("angle", 3)
     mul(angle[:, 0:3:2, :], twice(low[:]), twice(ratio[:]))
     mul(high[:], high[:], square_ratio[:])
@@ -317,8 +319,8 @@ def tile_unifiedautoencodernet_pa_t_kernel(tc, h_enc2, We3, be3, params, Wd1, bd
                     z_grouped[i] = stage.tile([P, CHUNK * PACK], BF16, align_bytes=64, name="z_grouped_i")
                 rows = slice(first * P, (first + count) * P)
                 copy(
-                    out=z_grouped[i][:, PACK * rows.start : PACK * rows.stop].rearrange("p (b i t) -> p b t i", i=4, t=PACK),
-                    in_=z_planes[i][:, :, rows].rearrange("p t (b i) -> p b t i", i=4),
+                    out=z_grouped[i][:, PACK * rows.start : PACK * rows.stop].rearrange("p (b i t) -> p b t i", i=RUN, t=PACK),
+                    in_=z_planes[i][:, :, rows].rearrange("p t (b i) -> p b t i", i=RUN),
                 )
 
         def quantise_z(i, first=0, count=BLOCKS):

@@ -340,27 +340,29 @@ def tile_unifiedautoencodernet_pa_t_kernel(tc, h_enc2, We3, be3, params, Wd1, bd
                 acc[i, r] = pool.tile([P, WIDTH], F32, tag=tag, name=tag)
                 product(acc[i, r][:], ("z", i), slice(r * P, (r + 1) * P), "wd1")
 
-        def add_bias(i, r):
+        def add_bias(i, r, columns=slice(0, WIDTH)):
             if exists(i) and r < PIECES[i][2]:
-                nc.vector.tensor_tensor(out=result[i][:, r, :], in0=acc[i, r][:], in1=bd1_rows[:], op=ALU.add)
+                nc.vector.tensor_tensor(
+                    out=result[i][:, r, columns], in0=acc[i, r][:, columns], in1=bd1_rows[:, columns], op=ALU.add
+                )
 
-        def relu_and_store(i, first, count, engine="gpsimd"):
+        def relu_and_store(i, first, count, engine="gpsimd", columns=slice(0, WIDTH)):
             if exists(i) and first < PIECES[i][2]:
                 chunk, start, blocks = PIECES[i]
                 pair = slice(first, min(first + count, blocks))
                 if engine == "scalar":
-                    nc.scalar.activation(out=result[i][:, pair, :], in_=result[i][:, pair, :], func=ACT.Relu)
+                    nc.scalar.activation(out=result[i][:, pair, columns], in_=result[i][:, pair, columns], func=ACT.Relu)
                 elif engine == "vector":
                     nc.vector.tensor_scalar(
-                        out=result[i][:, pair, :], in0=result[i][:, pair, :], scalar1=0.0, scalar2=None, op0=ALU.max
+                        out=result[i][:, pair, columns], in0=result[i][:, pair, columns], scalar1=0.0, scalar2=None, op0=ALU.max
                     )
                 else:
                     nc.gpsimd.tensor_scalar(
-                        out=result[i][:, pair, :], in0=result[i][:, pair, :], scalar1=FLT_MAX, scalar2=0.0,
+                        out=result[i][:, pair, columns], in0=result[i][:, pair, columns], scalar1=FLT_MAX, scalar2=0.0,
                         op0=ALU.min, op1=ALU.max,
                     )
                 chunk_out = out[chunk * CHUNK : (chunk + 1) * CHUNK, :].rearrange("(p r) j -> p r j", r=BLOCKS)
-                nc.sync.dma_start(out=chunk_out[:, start + pair.start : start + pair.stop, :], in_=result[i][:, pair, :])
+                nc.sync.dma_start(out=chunk_out[:, start + pair.start : start + pair.stop, columns], in_=result[i][:, pair, columns])
 
         we3_words = we3_rows[:].bitcast(F32)
         flip("we3", psum_out, "acc", BLOCKS, lambda n, u: we3_words[:, 256 * n + P * u : 256 * n + P * u + P])
@@ -378,7 +380,7 @@ def tile_unifiedautoencodernet_pa_t_kernel(tc, h_enc2, We3, be3, params, Wd1, bd
                 flip_piece(1)
             if point == 2:
                 quantise_piece(0)
-                for t in (3, 0, 1, 2):
+                for t in (0, 3, 1, 2):
                     first_product(0, t)
 
         amplitude, phase_turns, phase_rad, finish_constants = qubit_constants(nc, consts, angles, bias, quarter, w, between)
@@ -462,6 +464,9 @@ def tile_unifiedautoencodernet_pa_t_kernel(tc, h_enc2, We3, be3, params, Wd1, bd
             second_product(last, r, psum_theta, "theta")
             if r == 1:
                 regroup_z(last, 3, 1, nc.vector.tensor_copy)
-        for r in range(BLOCKS):
+        for r in range(BLOCKS - 1):
             add_bias(last, r)
             relu_and_store(last, r, 1, ("gpsimd", "scalar")[r % 2])
+        for columns in (slice(0, WIDTH // 2), slice(WIDTH // 2, WIDTH)):
+            add_bias(last, BLOCKS - 1, columns)
+            relu_and_store(last, BLOCKS - 1, 1, "scalar", columns)

@@ -28,6 +28,7 @@ HALF_PI = 0.5 * math.pi
 TINY = 2.0**-100
 FLT_MAX = 3.4028234663852886e38
 
+LOADS = 5
 RUN = 8
 GUESS = (1.0375891712, 0.3825653414, 3.8018101902, -6.0852806269, 2.4341122508)
 TURNS_PLANES = (3,)
@@ -160,7 +161,9 @@ def tile_unifiedautoencodernet_pa_t_kernel(tc, h_enc2, We3, be3, params, Wd1, bd
         tc.tile_pool(name="consts", bufs=1) as consts,
         tc.tile_pool(name="stage", bufs=2) as stage,
         tc.tile_pool(name="planes", bufs=4) as planes,
-        tc.tile_pool(name="results", bufs=4) as results,
+        tc.tile_pool(name="parts", bufs=8) as parts,
+        tc.tile_pool(name="loads", bufs=LOADS) as loads,
+        tc.tile_pool(name="results", bufs=14) as results,
         tc.psum_pool(name="psum_flip", bufs=2) as psum_flip,
         tc.psum_pool(name="psum_theta", bufs=4) as psum_theta,
         tc.psum_pool(name="psum_out", bufs=2) as psum_out,
@@ -177,18 +180,25 @@ def tile_unifiedautoencodernet_pa_t_kernel(tc, h_enc2, We3, be3, params, Wd1, bd
         we3_rows = consts.tile([P, PACK * WIDTH], BF16, name="we3_rows")
         wd1_rows = consts.tile([P, BLOCKS * WIDTH], BF16, name="wd1_rows")
         bd1_rows = consts.tile([P, WIDTH], BF16, name="bd1_rows")
-        h_rows = [consts.tile([P, BLOCKS * WIDTH], BF16, name="h_rows_%d" % c) for c in range(CHUNKS)]
-        nc.sync.dma_start(out=we3_rows[:], in_=We3.rearrange("(m t) k -> m (t k)", t=PACK))
-        for c in range(CHUNKS):
-            nc.sync.dma_start(
-                out=h_rows[c][:],
-                in_=h_enc2[c * CHUNK : (c + 1) * CHUNK, :].rearrange("(p r) k -> p (r k)", r=BLOCKS),
-            )
-            if c == 2:
+        h_rows = {}
+
+        def load(c):
+            if c < CHUNKS:
+                h_rows[c] = loads.tile([P, BLOCKS * WIDTH], BF16, name="h_rows_c")
                 nc.sync.dma_start(
-                    out=wd1_rows[:].rearrange("j (n q) -> j n q", n=BLOCKS), in_=Wd1.rearrange("(n j) q -> j n q", j=P)
+                    out=h_rows[c][:],
+                    in_=h_enc2[c * CHUNK : (c + 1) * CHUNK, :].rearrange("(p r) k -> p (r k)", r=BLOCKS),
                 )
-                nc.sync.dma_start(out=bd1_rows[:], in_=bd1.partition_broadcast(P))
+
+        nc.sync.dma_start(out=we3_rows[:], in_=We3.rearrange("(m t) k -> m (t k)", t=PACK))
+        for c in range(3):
+            load(c)
+        nc.sync.dma_start(
+            out=wd1_rows[:].rearrange("j (n q) -> j n q", n=BLOCKS), in_=Wd1.rearrange("(n j) q -> j n q", j=P)
+        )
+        nc.sync.dma_start(out=bd1_rows[:], in_=bd1.partition_broadcast(P))
+        for c in range(3, LOADS):
+            load(c)
 
         quarter = consts.tile([P, 2, LAYERS * PACK * 3], F32, name="quarter")
         nc.gpsimd.memset(quarter[:, 0, :], 0.0)
@@ -290,7 +300,7 @@ def tile_unifiedautoencodernet_pa_t_kernel(tc, h_enc2, We3, be3, params, Wd1, bd
 
         def part_of_turn(i, t):
             if exists(i):
-                part[i, t] = planes.tile([P, rows_of(i)], F32, tag="part", name="part")
+                part[i, t] = parts.tile([P, rows_of(i)], F32, tag="part", name="part")
                 nc.vector.scalar_tensor_tensor(
                     out=part[i, t][:], in0=theta[i, t][:], scalar=INV_TWO_PI, in1=whole[i, t][:],
                     op0=ALU.mult, op1=ALU.subtract,
@@ -346,23 +356,16 @@ def tile_unifiedautoencodernet_pa_t_kernel(tc, h_enc2, We3, be3, params, Wd1, bd
                     out=result[i][:, r, columns], in0=acc[i, r][:, columns], in1=bd1_rows[:, columns], op=ALU.add
                 )
 
-        def relu_and_store(i, first, count, engine="gpsimd", columns=slice(0, WIDTH)):
-            if exists(i) and first < PIECES[i][2]:
-                chunk, start, blocks = PIECES[i]
-                pair = slice(first, min(first + count, blocks))
+        def relu_and_store(i, first, count, engine="gpsimd"):
+            if exists(i):
+                columns = slice(int(first * WIDTH), int((first + count) * WIDTH))
+                values = result[i][:].rearrange("p r j -> p (r j)")[:, columns]
                 if engine == "scalar":
-                    nc.scalar.activation(out=result[i][:, pair, columns], in_=result[i][:, pair, columns], func=ACT.Relu)
-                elif engine == "vector":
-                    nc.vector.tensor_scalar(
-                        out=result[i][:, pair, columns], in0=result[i][:, pair, columns], scalar1=0.0, scalar2=None, op0=ALU.max
-                    )
+                    nc.scalar.activation(out=values, in_=values, func=ACT.Relu)
                 else:
-                    nc.gpsimd.tensor_scalar(
-                        out=result[i][:, pair, columns], in0=result[i][:, pair, columns], scalar1=FLT_MAX, scalar2=0.0,
-                        op0=ALU.min, op1=ALU.max,
-                    )
-                chunk_out = out[chunk * CHUNK : (chunk + 1) * CHUNK, :].rearrange("(p r) j -> p r j", r=BLOCKS)
-                nc.sync.dma_start(out=chunk_out[:, start + pair.start : start + pair.stop, columns], in_=result[i][:, pair, columns])
+                    nc.gpsimd.tensor_scalar(out=values, in0=values, scalar1=FLT_MAX, scalar2=0.0, op0=ALU.min, op1=ALU.max)
+                chunk_out = out[i * CHUNK : (i + 1) * CHUNK, :].rearrange("(p r) j -> p (r j)", r=BLOCKS)
+                nc.sync.dma_start(out=chunk_out[:, columns], in_=values)
 
         we3_words = we3_rows[:].bitcast(F32)
         flip("we3", psum_out, "acc", BLOCKS, lambda n, u: we3_words[:, 256 * n + P * u : 256 * n + P * u + P])
@@ -373,11 +376,13 @@ def tile_unifiedautoencodernet_pa_t_kernel(tc, h_enc2, We3, be3, params, Wd1, bd
                 copy_out("we3", 0)
                 copy_out("we3", 1)
                 flip_piece(0)
+                load(LOADS)
             if point == 1:
                 quantise("we3", grouped["we3"], consts, "we3")
                 copy_out_piece(0, 0)
                 copy_out_piece(0, 1)
                 flip_piece(1)
+                load(LOADS + 1)
             if point == 2:
                 quantise_piece(0)
                 for t in (0, 3, 1, 2):
@@ -435,6 +440,7 @@ def tile_unifiedautoencodernet_pa_t_kernel(tc, h_enc2, We3, be3, params, Wd1, bd
             if j == 0:
                 quantise("wd1", grouped["wd1"], consts, "wd1")
             regroup_z(j)
+            load(j + 3 + LOADS)
 
         last = CHUNKS - 1
         for t in (0, 1):
@@ -467,6 +473,6 @@ def tile_unifiedautoencodernet_pa_t_kernel(tc, h_enc2, We3, be3, params, Wd1, bd
         for r in range(BLOCKS - 1):
             add_bias(last, r)
             relu_and_store(last, r, 1, ("gpsimd", "scalar")[r % 2])
-        for columns in (slice(0, WIDTH // 2), slice(WIDTH // 2, WIDTH)):
-            add_bias(last, BLOCKS - 1, columns)
-            relu_and_store(last, BLOCKS - 1, 1, "scalar", columns)
+        for half in range(2):
+            add_bias(last, BLOCKS - 1, slice(half * WIDTH // 2, (half + 1) * WIDTH // 2))
+            relu_and_store(last, BLOCKS - 1 + 0.5 * half, 0.5, "scalar")

import math

import concourse.mybir as mybir
from concourse.masks import make_identity

F32 = mybir.dt.float32
BF16 = mybir.dt.bfloat16
I32 = mybir.dt.int32
U32 = mybir.dt.uint32
U8 = mybir.dt.uint8
FP8X4 = mybir.dt.float8_e4m3fn_x4
ALU = mybir.AluOpType
ACT = mybir.ActivationFunctionType

P = 128
PACK = 4
ROWS = 8192
WIDTH = 512
CHUNK = 512
BLOCKS = CHUNK // P
CHUNKS = ROWS // CHUNK
LAYERS = 2
RX, RY, RZ = 0, 1, 2

TWO_PI = 2.0 * math.pi
INV_TWO_PI = 1.0 / TWO_PI
HALF_PI = 0.5 * math.pi
TINY = 2.0**-100
FLT_MAX = 3.4028234663852886e38

LOADS = 5
RUN = 8
GUESS = (1.0375891712, 0.3825653414, 3.8018101902, -6.0852806269, 2.4341122508)
TURNS_PLANES = (3,)

PIECES = [(c, 0, BLOCKS) for c in range(CHUNKS)]

FLOPS = 2 * 2 * ROWS * WIDTH * WIDTH


def qubit_constants(nc, consts, angles, bias, quarter, w, between):
    def small(name, *dims):
        return consts.tile([P, *dims, PACK], F32, name=name)

    def mul(out, a, b):
        nc.vector.tensor_tensor(out=out, in0=a, in1=b, op=ALU.mult)

    def add(out, a, b):
        nc.vector.tensor_tensor(out=out, in0=a, in1=b, op=ALU.add)

    def sub(out, a, b):
        nc.vector.tensor_tensor(out=out, in0=a, in1=b, op=ALU.subtract)

    def twice(values):
        return values.unsqueeze(1).to_broadcast([P, 2, PACK])

    gates = LAYERS * PACK * 3
    turns = consts.tile([P, 2, gates], F32, name="turns")
    nearest = consts.tile([P, 2, gates], I32, name="nearest")
    for target in (nearest, turns):
        nc.vector.scalar_tensor_tensor(
            out=target[:], in0=angles[:].unsqueeze(1).to_broadcast([P, 2, gates]), scalar=INV_TWO_PI, in1=quarter[:],
            op0=ALU.mult, op1=ALU.add,
        )
    sub(turns[:], turns[:], nearest[:])
    trig_flat = consts.tile([P, 2, gates], F32, name="trig")
    nc.scalar.activation(out=trig_flat[:], in_=turns[:], func=ACT.Sin, scale=TWO_PI)
    between(0)
    trig = trig_flat[:].rearrange("p s (l t g) -> p s l t g", l=LAYERS, t=PACK)

    def sin(layer, gate):
        return trig[:, 0, layer, :, gate]

    def cos(layer, gate):
        return trig[:, 1, layer, :, gate]

    def both(layer, gate):
        return trig[:, :, layer, :, gate]

    u_yz, by_ux, by_uy, cx_y = [small(name, 2) for name in ("u_yz", "by_ux", "by_uy", "cx_y")]
    s_uz, p, q, c_p = [small(name) for name in ("s_uz", "p", "q", "c_p")]
    z_terms = consts.tile([P, PACK, 3], F32, name="z_terms")
    mul(u_yz[:], both(1, RX), twice(cos(1, RY)))
    mul(by_ux[:], both(0, RZ), twice(sin(1, RY)))
    mul(cx_y[:], both(0, RY), twice(cos(0, RX)))
    mul(by_uy[:], both(0, RZ), twice(u_yz[:, 0, :]))
    mul(s_uz[:], sin(0, RY), u_yz[:, 1, :])
    mul(z_terms[:, :, 0], cx_y[:, 1, :], u_yz[:, 1, :])
    sub(p[:], by_uy[:, 0, :], by_ux[:, 1, :])
    add(q[:], by_uy[:, 1, :], by_ux[:, 0, :])
    mul(c_p[:], cos(0, RY), p[:])
    mul(z_terms[:, :, 1], cx_y[:, 0, :], p[:])
    nc.vector.scalar_tensor_tensor(out=z_terms[:, :, 2], in0=q[:], scalar=-1.0, in1=sin(0, RX), op0=ALU.mult, op1=ALU.mult)
    sub(w[:, :, 0], c_p[:], s_uz[:])
    nc.vector.tensor_reduce(out=w[:, :, 1], in_=z_terms[:], axis=mybir.AxisListType.X, op=ALU.add)

    sign = small("sign")
    nc.vector.tensor_scalar(out=sign[:], in0=w[:, :, 0], scalar1=0.0, scalar2=0.5, op0=ALU.is_ge, op1=ALU.subtract)

    xy, size, total, share, ratio, square, low, high, square_ratio = [
        small("xy", 2), *[small(name) for name in ("size", "total", "share", "ratio", "square", "low", "high", "square_ratio")]
    ]
    nc.vector.tensor_reduce(
        out=total[:], in_=w[:], axis=mybir.AxisListType.X, op=ALU.add, apply_absolute_value=True
    )
    mul(xy[:], w[:, :, 0:2].rearrange("p t c -> p c t"), twice(sign[:]))
    nc.vector.scalar_tensor_tensor(out=size[:], in0=w[:, :, 1], scalar=-1.0, in1=w[:, :, 1], op0=ALU.mult, op1=ALU.max)
    nc.vector.reciprocal(out=total[:], in_=total[:])
    nc.vector.scalar_tensor_tensor(out=ratio[:], in0=xy[:, 1, :], scalar=2.0, in1=total[:], op0=ALU.mult, op1=ALU.mult)
    mul(share[:], size[:], total[:])
    mul(square[:], share[:], share[:])
    nc.vector.tensor_scalar(out=high[:], in0=share[:], scalar1=GUESS[3], scalar2=GUESS[2], op0=ALU.mult, op1=ALU.add)
    nc.vector.tensor_scalar(out=low[:], in0=share[:], scalar1=GUESS[1], scalar2=GUESS[0], op0=ALU.mult, op1=ALU.add)
    nc.vector.scalar_tensor_tensor(out=high[:], in0=square[:], scalar=GUESS[4], in1=high[:], op0=ALU.mult, op1=ALU.add)
    mul(square_ratio[:], square[:], ratio[:])
    between(1)
    angle = small("angle", 3)
    mul(angle[:, 0:3:2, :], twice(low[:]), twice(ratio[:]))
    mul(high[:], high[:], square_ratio[:])
    nc.vector.tensor_scalar(out=angle[:, 1, :], in0=angle[:, 0, :], scalar1=HALF_PI, scalar2=None, op0=ALU.add)
    add(angle[:], angle[:], high[:].unsqueeze(1).to_broadcast([P, 3, PACK]))
    sin_cos_sin = small("sin_cos_sin", 3)
    nc.scalar.activation(out=sin_cos_sin[:], in_=angle[:], func=ACT.Sin)
    between(2)
    bias_turns, base_turns = small("bias_turns"), small("base_turns")
    nc.vector.tensor_scalar(out=bias_turns[:], in0=bias[:], scalar1=INV_TWO_PI, scalar2=None, op0=ALU.mult)
    nc.vector.scalar_tensor_tensor(
        out=base_turns[:], in0=angle[:, 0, :], scalar=INV_TWO_PI, in1=bias_turns[:], op0=ALU.mult, op1=ALU.add
    )

    dot, cross = small("dot", 2), small("cross", 2)
    along, inverse, across, error = [small(name) for name in ("along", "inverse", "across", "error")]
    mul(dot[:], sin_cos_sin[:, 1:3, :], xy[:])
    mul(cross[:], sin_cos_sin[:, 0:2, :], xy[:])
    nc.vector.scalar_tensor_tensor(out=along[:], in0=dot[:, 0, :], scalar=TINY, in1=dot[:, 1, :], op0=ALU.add, op1=ALU.add)
    sub(across[:], cross[:, 1, :], cross[:, 0, :])
    nc.vector.reciprocal(out=inverse[:], in_=along[:])
    mul(error[:], across[:], inverse[:])
    phase_turns, phase_rad, amplitude = small("phase_turns"), small("phase_rad"), small("amplitude")

    def finish(step):
        if step == 0:
            nc.vector.tensor_scalar(out=phase_rad[:], in0=phase_turns[:], scalar1=TWO_PI, scalar2=None, op0=ALU.mult)
            nc.vector.scalar_tensor_tensor(
                out=across[:], in0=across[:], scalar=0.5, in1=error[:], op0=ALU.mult, op1=ALU.mult
            )
        if step == 1:
            add(along[:], along[:], across[:])
        if step == 2:
            nc.vector.scalar_tensor_tensor(out=amplitude[:], in0=along[:], scalar=4.0, in1=sign[:], op0=ALU.mult, op1=ALU.mult)

    nc.vector.scalar_tensor_tensor(
        out=phase_turns[:], in0=error[:], scalar=INV_TWO_PI, in1=base_turns[:], op0=ALU.mult, op1=ALU.add
    )
    return amplitude, phase_turns, phase_rad, finish


def tile_unifiedautoencodernet_pa_t_kernel(tc, h_enc2, We3, be3, params, Wd1, bd1, out):
    nc = tc.nc
    with (
        tc.tile_pool(name="consts", bufs=1) as consts,
        tc.tile_pool(name="stage", bufs=2) as stage,
        tc.tile_pool(name="planes", bufs=4) as planes,
        tc.tile_pool(name="parts", bufs=8) as parts,
        tc.tile_pool(name="loads", bufs=LOADS) as loads,
        tc.tile_pool(name="results", bufs=14) as results,
        tc.psum_pool(name="psum_flip", bufs=2) as psum_flip,
        tc.psum_pool(name="psum_theta", bufs=4) as psum_theta,
        tc.psum_pool(name="psum_out", bufs=2) as psum_out,
        tc.manual_schedule(),
    ):
        angles = consts.tile([P, LAYERS * PACK * 3], BF16, name="angles")
        bias = consts.tile([P, PACK], BF16, name="bias")
        with nc.allow_non_contiguous_dma(reason="a few bytes for each partition, once"):
            nc.sync.dma_start(
                out=angles[:].rearrange("p (l t a) -> p l t a", l=LAYERS, t=PACK),
                in_=params.rearrange("l (p t) a -> p l t a", t=PACK),
            )
            nc.scalar.dma_start(out=bias[:], in_=be3.rearrange("(p t) -> p t", t=PACK))
        we3_rows = consts.tile([P, PACK * WIDTH], BF16, name="we3_rows")
        wd1_rows = consts.tile([P, BLOCKS * WIDTH], BF16, name="wd1_rows")
        bd1_rows = consts.tile([P, WIDTH], BF16, name="bd1_rows")
        h_rows = {}

        def load(c):
            if c < CHUNKS:
                h_rows[c] = loads.tile([P, BLOCKS * WIDTH], BF16, name="h_rows_c")
                nc.sync.dma_start(
                    out=h_rows[c][:],
                    in_=h_enc2[c * CHUNK : (c + 1) * CHUNK, :].rearrange("(p r) k -> p (r k)", r=BLOCKS),
                )

        nc.sync.dma_start(out=we3_rows[:], in_=We3.rearrange("(m t) k -> m (t k)", t=PACK))
        for c in range(3):
            load(c)
        nc.sync.dma_start(
            out=wd1_rows[:].rearrange("j (n q) -> j n q", n=BLOCKS), in_=Wd1.rearrange("(n j) q -> j n q", j=P)
        )
        nc.sync.dma_start(out=bd1_rows[:], in_=bd1.partition_broadcast(P))
        for c in range(3, LOADS):
            load(c)

        quarter = consts.tile([P, 2, LAYERS * PACK * 3], F32, name="quarter")
        nc.gpsimd.memset(quarter[:, 0, :], 0.0)
        nc.gpsimd.memset(quarter[:, 1, :], 0.25)
        w = consts.tile([P, PACK, 3], F32, name="w")
        nc.vector.memset(w[:], TINY)
        warm = consts.tile([P, 1], F32, name="warm")
        nc.vector.memset(warm[:], 0.0)
        nc.scalar.activation(out=warm[:], in_=warm[:], func=ACT.Sin)
        identity = consts.tile([P, P], F32, name="identity")
        make_identity(nc, identity[:])

        flipped, grouped, codes_of, scales_of, theta, turns, whole, part, z_planes, z_grouped, acc, result, sines = [
            {} for n in range(13)
        ]

        def exists(i):
            return 0 <= i < len(PIECES)

        def rows_of(i):
            return PIECES[i][2] * P

        def flip(key, psum, tag, blocks, word_block):
            flipped[key] = []
            for first in range(0, blocks, 2):
                count = min(2, blocks - first)
                bank = psum.tile([P, count, 2, P], F32, tag=tag, name=tag)
                for n in range(count):
                    for u in range(2):
                        nc.tensor.transpose(bank[:, n, u, :], word_block(first + n, u), identity[:])
                flipped[key].append(bank)

        def copy_out(key, half):
            banks = flipped[key]
            count = banks[0][:].shape[1]
            if half == 0:
                width = count * len(banks) * P
                grouped[key] = stage.tile([P, width * PACK], BF16, align_bytes=64, tag="grouped%d" % width, name="grouped")
            words = grouped[key][:].bitcast(F32).rearrange("p (n c u) -> p n c u", c=P, u=2)
            nc.scalar.copy(
                out=words[:, count * half : count * (half + 1), :, :], in_=banks[half][:].rearrange("p n u c -> p n c u")
            )

        def quantise(key, source, pool, name):
            width = source[:].shape[1] // PACK
            codes = pool.tile([P, width], U32, align_bytes=64, name="%s_codes%d" % (name, width))
            scales = pool.tile([P, width], U8, align_bytes=64, name="%s_scales%d" % (name, width))
            nc.vector.quantize_mx(out=codes[:].bitcast(FP8X4), scales=scales[:], in_=source[:])
            codes_of[key], scales_of[key] = codes, scales

        def product(sums, left, left_columns, right):
            nc.tensor.matmul_mx(
                out=sums,
                lhsT=codes_of[left][:, left_columns].bitcast(FP8X4), lhsT_scale=scales_of[left][:, left_columns],
                rhs=codes_of[right][:].bitcast(FP8X4), rhs_scale=scales_of[right][:],
                start=True, stop=True,
            )

        def flip_piece(i):
            if exists(i):
                chunk, first, blocks = PIECES[i]
                words = h_rows[chunk][:].bitcast(F32)
                flip(i, psum_flip, "flipped", blocks,
                     lambda n, u: words[:, 256 * (first + n) + P * u : 256 * (first + n) + P * u + P])

        def copy_out_piece(i, half):
            if exists(i) and half < len(flipped[i]):
                copy_out(i, half)

        def quantise_piece(i):
            if exists(i) and i not in codes_of:
                quantise(i, grouped[i], stage, "h")

        def first_product(i, t):
            if exists(i) and (i, t) not in theta:
                theta[i, t] = psum_theta.tile([P, rows_of(i)], F32, tag="theta", name="theta")
                product(theta[i, t][:], "we3", slice(t * P, (t + 1) * P), i)

        def turns_of(i, t):
            if exists(i):
                turns[i, t] = planes.tile([P, rows_of(i)], F32, tag="turns", name="turns_t")
                nc.scalar.activation(
                    out=turns[i, t][:], in_=theta[i, t][:], func=ACT.Identity, scale=INV_TWO_PI, bias=phase_turns[:, t : t + 1]
                )

        def whole_turns(i, t):
            if exists(i):
                if t in TURNS_PLANES:
                    whole[i, t] = planes.tile([P, rows_of(i)], I32, tag="whole_g", name="whole_g")
                    nc.gpsimd.tensor_scalar(
                        out=whole[i, t][:], in0=turns[i, t][:], scalar1=1.0, scalar2=0.0, op0=ALU.mult, op1=ALU.add
                    )
                else:
                    whole[i, t] = planes.tile([P, rows_of(i)], I32, tag="whole", name="whole")
                    nc.vector.tensor_scalar(
                        out=whole[i, t][:], in0=theta[i, t][:], scalar1=INV_TWO_PI, scalar2=phase_turns[:, t : t + 1],
                        op0=ALU.mult, op1=ALU.add,
                    )

        def part_of_turn(i, t):
            if exists(i):
                part[i, t] = parts.tile([P, rows_of(i)], F32, tag="part", name="part")
                nc.vector.scalar_tensor_tensor(
                    out=part[i, t][:], in0=theta[i, t][:], scalar=INV_TWO_PI, in1=whole[i, t][:],
                    op0=ALU.mult, op1=ALU.subtract,
                )

        def sine_wave(i, t):
            if exists(i):
                if t == 0:
                    z_planes[i] = stage.tile([P, PACK, rows_of(i)], BF16, tag="z_planes%d" % rows_of(i), name="z_planes_i")
                sine = planes.tile([P, rows_of(i)], F32, tag="sine", name="sine")
                nc.scalar.activation(
                    out=sine[:], in_=part[i, t][:], func=ACT.Sin, scale=TWO_PI, bias=phase_rad[:, t : t + 1]
                )
                sines[i, t] = sine

        def multiply(i, t, engine=nc.gpsimd):
            if exists(i):
                engine.tensor_scalar(
                    out=z_planes[i][:, t, :], in0=sines[i, t][:], scalar1=amplitude[:, t : t + 1], scalar2=0.0,
                    op0=ALU.mult, op1=ALU.add,
                )

        def regroup_z(i, first=0, count=BLOCKS, copy=nc.scalar.copy):
            if exists(i):
                if first == 0:
                    z_grouped[i] = stage.tile([P, CHUNK * PACK], BF16, align_bytes=64, name="z_grouped_i")
                rows = slice(first * P, (first + count) * P)
                copy(
                    out=z_grouped[i][:, PACK * rows.start : PACK * rows.stop].rearrange("p (b i t) -> p b t i", i=RUN, t=PACK),
                    in_=z_planes[i][:, :, rows].rearrange("p t (b i) -> p b t i", i=RUN),
                )

        def quantise_z(i, first=0, count=BLOCKS):
            if exists(i):
                if first == 0:
                    codes_of["z", i] = stage.tile([P, CHUNK], U32, align_bytes=64, name="z_codes")
                    scales_of["z", i] = stage.tile([P, CHUNK], U8, align_bytes=64, name="z_scales")
                    result[i] = results.tile([P, BLOCKS, WIDTH], F32, name="result_i")
                rows = slice(first * P, (first + count) * P)
                nc.vector.quantize_mx(
                    out=codes_of["z", i][:, rows].bitcast(FP8X4), scales=scales_of["z", i][:, rows],
                    in_=z_grouped[i][:, PACK * rows.start : PACK * rows.stop],
                )

        def second_product(i, r, pool=psum_out, tag="acc"):
            if exists(i) and r < PIECES[i][2]:
                acc[i, r] = pool.tile([P, WIDTH], F32, tag=tag, name=tag)
                product(acc[i, r][:], ("z", i), slice(r * P, (r + 1) * P), "wd1")

        def add_bias(i, r, columns=slice(0, WIDTH)):
            if exists(i) and r < PIECES[i][2]:
                nc.vector.tensor_tensor(
                    out=result[i][:, r, columns], in0=acc[i, r][:, columns], in1=bd1_rows[:, columns], op=ALU.add
                )

        def relu_and_store(i, first, count, engine="gpsimd"):
            if exists(i):
                columns = slice(int(first * WIDTH), int((first + count) * WIDTH))
                values = result[i][:].rearrange("p r j -> p (r j)")[:, columns]
                if engine == "scalar":
                    nc.scalar.activation(out=values, in_=values, func=ACT.Relu)
                else:
                    nc.gpsimd.tensor_scalar(out=values, in0=values, scalar1=FLT_MAX, scalar2=0.0, op0=ALU.min, op1=ALU.max)
                chunk_out = out[i * CHUNK : (i + 1) * CHUNK, :].rearrange("(p r) j -> p (r j)", r=BLOCKS)
                nc.sync.dma_start(out=chunk_out[:, columns], in_=values)

        we3_words = we3_rows[:].bitcast(F32)
        flip("we3", psum_out, "acc", BLOCKS, lambda n, u: we3_words[:, 256 * n + P * u : 256 * n + P * u + P])
        wd1_words = wd1_rows[:].bitcast(F32)

        def between(point):
            if point == 0:
                copy_out("we3", 0)
                copy_out("we3", 1)
                flip_piece(0)
                load(LOADS)
            if point == 1:
                quantise("we3", grouped["we3"], consts, "we3")
                copy_out_piece(0, 0)
                copy_out_piece(0, 1)
                flip_piece(1)
                load(LOADS + 1)
            if point == 2:
                quantise_piece(0)
                for t in (0, 3, 1, 2):
                    first_product(0, t)

        amplitude, phase_turns, phase_rad, finish_constants = qubit_constants(nc, consts, angles, bias, quarter, w, between)

        for j in range(-1, CHUNKS - 1):
            copy_out_piece(j + 2, 0)
            for t in (0, 1):
                sine_wave(j, t)
                multiply(j, t)
            quantise_z(j - 1)
            second_product(j - 1, 0)
            second_product(j - 1, 1)
            quantise_piece(j + 1)
            if j == 0:
                flip("wd1", psum_out, "acc", BLOCKS, lambda n, u: wd1_words[:, 256 * n + u : 256 * n + 256 : 2])
            first_product(j + 1, 0)
            copy_out_piece(j + 2, 1)
            for t in (3, 2):
                part_of_turn(j, t)
                sine_wave(j, t)
                multiply(j, t)
            first_product(j + 1, 3)
            first_product(j + 1, 1)
            add_bias(j - 1, 0)
            second_product(j - 1, 2)
            relu_and_store(j - 1, 0, 1, "scalar")
            add_bias(j - 1, 1)
            second_product(j - 1, 3)
            first_product(j + 1, 2)
            flip_piece(j + 3)
            if j == 0:
                copy_out("wd1", 0)
            turns_of(j + 1, 3)
            whole_turns(j + 1, 3)
            if j == 0:
                copy_out("wd1", 1)
            relu_and_store(j - 1, 1, 1, "scalar")
            if j == -1:
                finish_constants(0)
            whole_turns(j + 1, 0)
            whole_turns(j + 1, 1)
            add_bias(j - 1, 2)
            add_bias(j - 1, 3)
            relu_and_store(j - 1, 2, 2)
            part_of_turn(j + 1, 0)
            part_of_turn(j + 1, 1)
            if j == -1:
                finish_constants(1)
            whole_turns(j + 1, 2)
            if j == -1:
                finish_constants(2)
            if j == 0:
                quantise("wd1", grouped["wd1"], consts, "wd1")
            regroup_z(j)
            load(j + 3 + LOADS)

        last = CHUNKS - 1
        for t in (0, 1):
            sine_wave(last, t)
            multiply(last, t)
        quantise_z(last - 1)
        second_product(last - 1, 0)
        second_product(last - 1, 1)
        for t in (3, 2):
            part_of_turn(last, t)
            sine_wave(last, t)
        add_bias(last - 1, 0)
        second_product(last - 1, 2)
        multiply(last, 3, nc.vector)
        multiply(last, 2, nc.vector)
        add_bias(last - 1, 1)
        second_product(last - 1, 3)
        relu_and_store(last - 1, 0, 2)
        regroup_z(last, 0, 1)
        regroup_z(last, 1, 1, nc.vector.tensor_copy)
        regroup_z(last, 2, 1)
        add_bias(last - 1, 2)
        add_bias(last - 1, 3)
        relu_and_store(last - 1, 2, 2, "scalar")
        for r in range(BLOCKS):
            quantise_z(last, r, 1)
            second_product(last, r, psum_theta, "theta")
            if r == 1:
                regroup_z(last, 3, 1, nc.vector.tensor_copy)
        for r in range(BLOCKS - 1):
            add_bias(last, r)
            relu_and_store(last, r, 1, ("gpsimd", "scalar")[r % 2])
        for half in range(2):
            add_bias(last, BLOCKS - 1, slice(half * WIDTH // 2, (half + 1) * WIDTH // 2))
            relu_and_store(last, BLOCKS - 1 + 0.5 * half, 0.5, "scalar")
